import numpy as np
import ml_dtypes


def mxq(x, axis, fmt="e4m3"):
    dtype, down = {"e4m3": (ml_dtypes.float8_e4m3fn, 7), "e5m2": (ml_dtypes.float8_e5m2, 14)}[fmt]
    v = np.moveaxis(np.asarray(x, np.float32).astype(ml_dtypes.bfloat16).astype(np.float64), axis, -1)
    blocks = v.reshape(v.shape[:-1] + (-1, 32))
    amax = np.abs(blocks).max(-1, keepdims=True)
    byte = np.maximum(np.where(amax > 0, np.frexp(amax)[1] - 1 + 127, 0) - down, 1)
    scale = np.exp2(byte - 127.0)
    codes = (blocks / scale).astype(np.float32).astype(dtype).astype(np.float64)
    return np.moveaxis((codes * scale).reshape(v.shape), -1, axis)


WIDE = False


def mx_kscale(k):
    if not WIDE:
        return np.ones(k)
    levels = np.array([10, -10, 5, -5, 0])
    a = np.random.permutation(np.resize(levels, k // 512 * 4)).reshape(k // 512, 4)
    idx = np.arange(k)
    return np.exp2(a[idx // 512, idx % 128 // 32])


BF16 = ml_dtypes.bfloat16


def bf(x):
    return np.asarray(x, np.float32).astype(BF16)


def f64(x):
    return np.asarray(x).astype(np.float64)


N, M, C, C0, C1 = 256, 64, 128, 512, 512
EPS = 1e-3


def bn_relu(y, gamma, beta):
    mean = y.mean(axis=(0, 1))
    var = y.var(axis=(0, 1))
    return np.maximum((y - mean) * (1.0 / np.sqrt(var + EPS)) * gamma + beta, 0.0)


def setup_inputs():
    t = mx_kscale(C0)
    r0 = 0.05 * 4.0 ** np.random.random(C0)
    return {"voxel_feats": bf(np.random.standard_normal((N, M, C)) + 0.5 * np.random.standard_normal(C)),
            "W0": bf(np.random.standard_normal((C0, C)) / np.sqrt(C) * r0[:, None]),
            "gamma0": bf((1.0 + 0.1 * np.random.standard_normal(C0)) * t),
            "beta0": bf(0.2 * np.random.standard_normal(C0) * t),
            "W1": bf(np.random.standard_normal((C1, 2 * C0)) * 0.2 / np.sqrt(2 * C0) / np.concatenate([t, t])[None, :]),
            "gamma1": bf(1.0 + 0.1 * np.random.standard_normal(C1)),
            "beta1": bf(0.3 * np.random.standard_normal(C1) - 0.5)}


def reference(voxel_feats, W0, gamma0, beta0, W1, gamma1, beta1):
    y0 = f64(voxel_feats) @ f64(W0).T
    p = bn_relu(y0, f64(gamma0), f64(beta0))
    a = p.max(axis=1)
    w1q = mxq(f64(W1).T, 0, "e4m3")
    y1 = (mxq(p, 2, "e4m3") @ w1q[:C0]) + (mxq(a, 1, "e4m3") @ w1q[C0:])[:, None, :]
    return bn_relu(y1, f64(gamma1), f64(beta1)).max(axis=1)

@@ -1,0 +1,289 @@
+from contextlib import ExitStack
+
+import concourse.mybir as mybir
+from concourse.masks import make_identity
+
+FP8X4 = mybir.dt.float8_e4m3fn_x4
+BF16 = mybir.dt.bfloat16
+F32 = mybir.dt.float32
+U32 = mybir.dt.uint32
+U8 = mybir.dt.uint8
+ACT = mybir.ActivationFunctionType
+ALU = mybir.AluOpType
+AX = mybir.AxisListType
+
+P = 128
+NVOX = 256
+NPTS = 64
+ROWS = NVOX * NPTS
+EPS = 1e-3
+NBLK = 32
+BPG = 16
+
+FLOPS = 2 * (ROWS * 128 * 512 + ROWS * 512 * 512 + NVOX * 512 * 512)
+
+
+def tile_vfe_t_kernel(tc, voxel_feats, W0, gamma0, beta0, W1, gamma1, beta1, out):
+    nc = tc.nc
+    with ExitStack() as ctx:
+        keep = ctx.enter_context(tc.tile_pool(name="keep", bufs=1))
+        work = ctx.enter_context(tc.tile_pool(name="work", bufs=3))
+        psum = ctx.enter_context(tc.psum_pool(name="psum", bufs=1))
+
+        def ps_a(shape, dtype, name):
+            return psum.tile(shape, dtype, name=name, tag="a", bufs=3)
+
+        def ps_b(shape, dtype, name):
+            return psum.tile(shape, dtype, name=name, tag="b", bufs=4)
+
+        def ps_c(shape, dtype, name):
+            return psum.tile(shape, dtype, name=name, tag="c", bufs=1)
+
+        x_sb = keep.tile([P, 2, NPTS, 128], BF16, name="x_sb")
+        xv = voxel_feats.rearrange("(g n) m c -> n g m c", g=2)
+        for g in range(2):
+            for q in range(4):
+                nc.sync.dma_start(out=x_sb[:, g, 16 * q:16 * (q + 1), :], in_=xv[:, g, 16 * q:16 * (q + 1), :])
+        w1_sb = keep.tile([P, 4, 1024], BF16, name="w1_sb")
+        w1v = W1.rearrange("(ct i) k -> i ct k", ct=4)
+        for hh in range(2):
+            nc.sync.dma_start(out=w1_sb[:, 2 * hh:2 * hh + 2, :], in_=w1v[:, 2 * hh:2 * hh + 2, :])
+
+        w0_sb = keep.tile([P, 4, 128], BF16, name="w0_sb")
+        nc.scalar.dma_start(out=w0_sb[:], in_=W0.rearrange("(j t) c -> j t c", t=4))
+        g0_bf = keep.tile([P, 4], BF16, name="g0_bf")
+        nc.scalar.dma_start(out=g0_bf[:], in_=gamma0.rearrange("(j t) -> j t", t=4))
+        b0_bf = keep.tile([P, 4], BF16, name="b0_bf")
+        nc.scalar.dma_start(out=b0_bf[:], in_=beta0.rearrange("(j t) -> j t", t=4))
+        gb1_rows = keep.tile([P, P], BF16, name="gb1_rows")
+        nc.vector.memset(gb1_rows[:], 0.0)
+        nc.scalar.dma_start(out=gb1_rows[0:4, :], in_=gamma1.rearrange("(r i) -> r i", r=4))
+        nc.scalar.dma_start(out=gb1_rows[4:8, :], in_=beta1.rearrange("(r i) -> r i", r=4))
+
+        one_col = keep.tile([P, 1], F32, name="one_col")
+        nc.vector.memset(one_col[:], 1.0)
+        warm = keep.tile([P, 1], F32, name="warm")
+        nc.scalar.activation(out=warm[:], in_=one_col[:], func=ACT.Sqrt)
+        ident_bf = keep.tile([P, P], BF16, name="ident_bf")
+        make_identity(nc, ident_bf[:])
+        ident_f = keep.tile([P, P], F32, name="ident_f")
+        make_identity(nc, ident_f[:])
+        pick = keep.tile([P, 2], F32, name="pick")
+        nc.vector.memset(pick[:], 0.0)
+        nc.vector.memset(pick[:, 0:1], 1.0)
+        gs = keep.tile([P, 130], F32, name="gs")
+        nc.vector.memset(gs[:, 128:130], 0.0)
+
+        w0t_ps = ps_a([P, 4, P], BF16, "w0t_ps")
+        for t in range(4):
+            nc.tensor.transpose(w0t_ps[:, t, :], w0_sb[:, t, :], ident_bf[:])
+        w0t = keep.tile([P, 4, P], BF16, name="w0t")
+        nc.vector.tensor_copy(out=w0t[:], in_=w0t_ps[:])
+        w0t_f = keep.tile([P, 4, P], F32, name="w0t_f")
+        nc.vector.tensor_copy(out=w0t_f[:], in_=w0t_ps[:])
+        w0_f = keep.tile([P, 4, P], F32, name="w0_f")
+        nc.vector.tensor_copy(out=w0_f[:], in_=w0_sb[:])
+        g0 = keep.tile([P, 4], F32, name="g0")
+        nc.vector.tensor_copy(out=g0[:], in_=g0_bf[:])
+        be0 = keep.tile([P, 4], F32, name="be0")
+        nc.vector.tensor_copy(out=be0[:], in_=b0_bf[:])
+
+        gb1_ps = ps_a([P, P], BF16, "gb1_ps")
+        nc.tensor.transpose(gb1_ps[:], gb1_rows[:], ident_bf[:])
+        gb1 = keep.tile([P, 8], F32, name="gb1")
+        nc.vector.tensor_copy(out=gb1[:], in_=gb1_ps[:, 0:8])
+        pos = keep.tile([P, 4], F32, name="pos")
+        nc.vector.tensor_scalar(out=pos[:], in0=gb1[:, 0:4], scalar1=0.0, scalar2=None, op0=ALU.is_gt)
+        neg = keep.tile([P, 4], F32, name="neg")
+        nc.vector.tensor_scalar(out=neg[:], in0=gb1[:, 0:4], scalar1=0.0, scalar2=None, op0=ALU.is_lt)
+        sgn = keep.tile([P, 4], F32, name="sgn")
+        nc.vector.tensor_tensor(out=sgn[:], in0=pos[:], in1=neg[:], op=ALU.subtract)
+
+        g_ps = ps_c([P, P], F32, "g_ps")
+        xt = keep.tile([P, NBLK, 512], BF16, name="xt")
+        sx_s = keep.tile([P, BPG], F32, name="sx_s")
+        sx_v = keep.tile([P, BPG], F32, name="sx_v")
+        for b in range(NBLK):
+            g, mb = divmod(b, BPG)
+            xt_ps = ps_b([P, 4, P], BF16, "xt_ps")
+            for mi in range(4):
+                xm = x_sb[:, g, 4 * mb + mi, :]
+                nc.tensor.transpose(xt_ps[:, mi, :], xm, ident_bf[:])
+                nc.tensor.matmul(g_ps[:], lhsT=xm, rhs=xm, start=(b == 0 and mi == 0), stop=(b == NBLK - 1 and mi == 3))
+            flat = xt_ps[:].rearrange("p a r -> p (a r)")
+            if b % 2 == 0:
+                nc.scalar.activation(out=xt[:, b, :], in_=flat, func=ACT.Copy, accum_out=sx_s[:, b // 2:b // 2 + 1])
+            else:
+                nc.vector.tensor_scalar(out=xt[:, b, :], in0=flat, scalar1=1.0, scalar2=None, op0=ALU.mult,
+                                        op1=ALU.add, accum_out=sx_v[:, b // 2:b // 2 + 1])
+
+        w1w = w1_sb[:].bitcast(F32)
+        w1g = keep.tile([P, 2, 512, 4], BF16, name="w1g", align_bytes=64)
+        w1gw = w1g[:].bitcast(F32)
+        w1c = keep.tile([P, 2, 512], U32, name="w1c", align_bytes=64)
+        w1s = keep.tile([P, 2, 512], U8, name="w1s", align_bytes=64)
+        for h in range(2):
+            for cp in range(2):
+                wt_ps = ps_a([P, 2, 2, P], F32, "wt_ps")
+                for u in range(2):
+                    for cc in range(2):
+                        nc.tensor.transpose(wt_ps[:, u, cc, :], w1w[:, 2 * cp + cc, 256 * h + u:256 * h + 256:2], ident_f[:])
+                nc.vector.tensor_copy(out=w1gw[:, h, 256 * cp:256 * (cp + 1), :],
+                                      in_=wt_ps[:].rearrange("p u c i -> p (c i) u"))
+        for h in range(2):
+            nc.vector.quantize_mx(out=w1c[:, h, :].bitcast(FP8X4), scales=w1s[:, h, :],
+                                  in_=w1g[:, h, :, :].rearrange("p c t -> p (c t)"))
+
+        nc.vector.tensor_copy(out=gs[:, 0:128], in_=g_ps[:])
+        sxa = keep.tile([P, 1], F32, name="sxa")
+        nc.vector.tensor_reduce(out=sxa[:], in_=sx_s[:], axis=AX.X, op=ALU.add)
+        sxb = keep.tile([P, 1], F32, name="sxb")
+        nc.vector.tensor_reduce(out=sxb[:], in_=sx_v[:], axis=AX.X, op=ALU.add)
+        nc.vector.tensor_tensor(out=gs[:, 128:129], in0=sxa[:], in1=sxb[:], op=ALU.add)
+        prod = keep.tile([P, 4, P], F32, name="prod")
+        mean0 = keep.tile([P, 4], F32, name="mean0")
+        for h in range(2):
+            tq = ps_a([P, 2, 130], F32, "tq")
+            for tt in range(2):
+                nc.tensor.matmul(tq[:, tt, :], lhsT=w0t_f[:, 2 * h + tt, :], rhs=gs[:], start=True, stop=True)
+            nc.vector.tensor_tensor(out=prod[:, 2 * h:2 * h + 2, :], in0=tq[:, :, 0:128], in1=w0_f[:, 2 * h:2 * h + 2, :], op=ALU.mult)
+            nc.vector.tensor_scalar(out=mean0[:, 2 * h:2 * h + 2], in0=tq[:, :, 128], scalar1=1.0 / ROWS, scalar2=None, op0=ALU.mult)
+        q0 = keep.tile([P, 4], F32, name="q0")
+        nc.vector.tensor_reduce(out=q0[:], in_=prod[:], axis=AX.X, op=ALU.add)
+
+        def scale_and_shift(sumsq, mean, gam, bet, label):
+            msq = keep.tile([P, 4], F32, name="msq" + label)
+            nc.vector.tensor_tensor(out=msq[:], in0=mean, in1=mean, op=ALU.mult)
+            var = keep.tile([P, 4], F32, name="var" + label)
+            nc.vector.scalar_tensor_tensor(out=var[:], in0=sumsq, scalar=1.0 / ROWS, in1=msq[:], op0=ALU.mult, op1=ALU.subtract)
+            nc.vector.tensor_scalar(out=var[:], in0=var[:], scalar1=0.0, scalar2=EPS, op0=ALU.max, op1=ALU.add)
+            std = keep.tile([P, 4], F32, name="std" + label)
+            nc.scalar.activation(out=std[:], in_=var[:], func=ACT.Sqrt)
+            rstd = keep.tile([P, 4], F32, name="rstd" + label)
+            nc.vector.reciprocal(out=rstd[:], in_=std[:])
+            scl = keep.tile([P, 4], F32, name="scl" + label)
+            nc.vector.tensor_tensor(out=scl[:], in0=gam, in1=rstd[:], op=ALU.mult)
+            msc = keep.tile([P, 4], F32, name="msc" + label)
+            nc.vector.tensor_tensor(out=msc[:], in0=mean, in1=scl[:], op=ALU.mult)
+            sft = keep.tile([P, 4], F32, name="sft" + label)
+            nc.vector.tensor_tensor(out=sft[:], in0=bet, in1=msc[:], op=ALU.subtract)
+            return scl, sft
+
+        s0, b0 = scale_and_shift(q0[:], mean0[:], g0[:], be0[:], "0")
+
+        ssq = keep.tile([P, 4, NBLK], F32, name="ssq")
+        rmax = [[keep.tile([P, 512], F32, name="rmax%d%d" % (g, ct)) for ct in range(4)] for g in range(2)]
+        rm = keep.tile([P, 4, 2, P], F32, name="rm")
+        arun = [keep.tile([P, 4, 512], BF16, name="arun%d" % g) for g in range(2)]
+        agr = keep.tile([P, 2, 512], BF16, name="agr", align_bytes=64)
+        ac = keep.tile([P, 2, P], U32, name="ac", align_bytes=64)
+        asc = keep.tile([P, 2, P], U8, name="asc", align_bytes=64)
+        e1 = [keep.tile([P, 512], F32, name="e1_%d" % g) for g in range(2)]
+        e2 = [keep.tile([P, 512], F32, name="e2_%d" % g) for g in range(2)]
+        prev_gr = None
+        zs_ps = None
+        for b in range(NBLK):
+            g, mb = divmod(b, BPG)
+            pt = work.tile([P, 4, 512], BF16, name="pt")
+            for t in range(4):
+                y0 = ps_a([P, 512], F32, "y0")
+                nc.tensor.matmul(y0[:], lhsT=w0t[:, t, :], rhs=xt[:, b, :], start=True, stop=True)
+                nc.scalar.activation(out=pt[:, t, :], in_=y0[:], func=ACT.Relu, bias=b0[:, t:t + 1], scale=s0[:, t:t + 1])
+            gr = work.tile([P, 512, 4], BF16, name="gr", align_bytes=64)
+            nc.vector.tensor_copy(out=gr[:].rearrange("p (c i) t -> p c t i", i=4),
+                                  in_=pt[:].rearrange("p t (c i) -> p c t i", i=4))
+            grf = gr[:].rearrange("p r t -> p (r t)")
+            codes = work.tile([P, 512], U32, name="codes", align_bytes=64)
+            scales = work.tile([P, 512], U8, name="scales", align_bytes=64)
+            nc.vector.quantize_mx(out=codes[:].bitcast(FP8X4), scales=scales[:], in_=grf)
+            arf = arun[g][:].rearrange("p a r -> p (a r)")
+            if mb == 1:
+                nc.vector.tensor_tensor(out=arf, in0=prev_gr, in1=grf, op=ALU.max)
+            elif mb > 1:
+                nc.vector.tensor_tensor(out=arf, in0=arf, in1=grf, op=ALU.max)
+            prev_gr = grf
+
+            for ct in range(4):
+                z = ps_b([P, 512], F32, "z")
+                nc.tensor.matmul_mx(out=z[:], lhsT=w1c[:, 0, ct * P:(ct + 1) * P].bitcast(FP8X4),
+                                    lhsT_scale=w1s[:, 0, ct * P:(ct + 1) * P],
+                                    rhs=codes[:].bitcast(FP8X4), rhs_scale=scales[:], start=True, stop=True)
+                junk = work.tile([P, 512], BF16, name="junk")
+                nc.scalar.activation(out=junk[:], in_=z[:], func=ACT.Square, accum_out=ssq[:, ct, b:b + 1])
+                if mb == 0:
+                    nc.vector.tensor_scalar(out=rmax[g][ct][:], in0=z[:], scalar1=sgn[:, ct:ct + 1], scalar2=None, op0=ALU.mult)
+                else:
+                    nc.vector.scalar_tensor_tensor(out=rmax[g][ct][:], in0=z[:], scalar=sgn[:, ct:ct + 1],
+                                                   in1=rmax[g][ct][:], op0=ALU.mult, op1=ALU.max)
+            if mb == 0:
+                zs_ps = ps_c([P, 512], F32, "zs_ps")
+            for mi in range(4):
+                nc.tensor.matmul_mx(out=zs_ps[:], lhsT=codes[:, mi * P:(mi + 1) * P].bitcast(FP8X4),
+                                    lhsT_scale=scales[:, mi * P:(mi + 1) * P],
+                                    rhs=w1c[:, 0, :].bitcast(FP8X4), rhs_scale=w1s[:, 0, :],
+                                    start=(mb == 0 and mi == 0), stop=(mb == BPG - 1 and mi == 3))
+
+            if mb == BPG - 1:
+                zs = work.tile([P, 512], F32, name="zs")
+                nc.vector.tensor_copy(out=zs[:], in_=zs_ps[:])
+                a1 = work.tile([P, 2, 512], BF16, name="a1")
+                nc.vector.tensor_tensor(out=a1[:], in0=arun[g][:, 0:2, :], in1=arun[g][:, 2:4, :], op=ALU.max)
+                nc.vector.tensor_tensor(out=agr[:, g, :], in0=a1[:, 0, :], in1=a1[:, 1, :], op=ALU.max)
+                nc.vector.quantize_mx(out=ac[:, g, :].bitcast(FP8X4), scales=asc[:, g, :], in_=agr[:, g, :])
+                u_ps = ps_a([P, 512], F32, "u_ps")
+                nc.tensor.matmul_mx(out=u_ps[:], lhsT=ac[:, g, :].bitcast(FP8X4), lhsT_scale=asc[:, g, :],
+                                    rhs=w1c[:, 1, :].bitcast(FP8X4), rhs_scale=w1s[:, 1, :], start=True, stop=True)
+                nc.vector.scalar_tensor_tensor(out=e1[g][:], in0=u_ps[:], scalar=float(NPTS), in1=zs[:], op0=ALU.mult, op1=ALU.add)
+                t2 = work.tile([P, 512], F32, name="t2")
+                nc.vector.tensor_tensor(out=t2[:], in0=e1[g][:], in1=zs[:], op=ALU.add)
+                nc.vector.tensor_tensor(out=e2[g][:], in0=u_ps[:], in1=t2[:], op=ALU.mult)
+                for ct in range(4):
+                    nc.vector.tensor_reduce(out=rm[:, ct, g, :], in_=rmax[g][ct][:].rearrange("p (a n) -> p n a", a=4),
+                                            axis=AX.X, op=ALU.max)
+
+        sum_ps = ps_a([P, 2, 4, 2, 2], F32, "sum_ps")
+        for g in range(2):
+            for qi in range(2):
+                src = e1[g] if qi == 0 else e2[g]
+                for ct in range(4):
+                    nc.tensor.matmul(sum_ps[:, qi, ct, g, :], lhsT=src[:, ct * P:(ct + 1) * P], rhs=pick[:], start=True, stop=True)
+        st = keep.tile([P, 2, 4], F32, name="st")
+        nc.vector.tensor_reduce(out=st[:].rearrange("p q c -> p (q c)"), in_=sum_ps[:].rearrange("p q c g k -> p (q c) (g k)"),
+                                axis=AX.X, op=ALU.add)
+        ssqt = keep.tile([P, 4], F32, name="ssqt")
+        nc.vector.tensor_reduce(out=ssqt[:], in_=ssq[:], axis=AX.X, op=ALU.add)
+        q1 = keep.tile([P, 4], F32, name="q1")
+        nc.vector.tensor_tensor(out=q1[:], in0=ssqt[:], in1=st[:, 1, :], op=ALU.add)
+        mean1 = keep.tile([P, 4], F32, name="mean1")
+        nc.vector.tensor_scalar(out=mean1[:], in0=st[:, 0, :], scalar1=1.0 / ROWS, scalar2=None, op0=ALU.mult)
+        s1, b1 = scale_and_shift(q1[:], mean1[:], gb1[:, 0:4], gb1[:, 4:8], "1")
+        s1abs = keep.tile([P, 4], F32, name="s1abs")
+        nc.vector.tensor_tensor(out=s1abs[:], in0=s1[:], in1=sgn[:], op=ALU.mult)
+
+        acf = ac[:].rearrange("p g n -> p (g n)")
+        ascf = asc[:].rearrange("p g n -> p (g n)")
+        fin = keep.tile([P, 4, 2, P], F32, name="fin")
+        for cp in range(2):
+            ut = ps_b([P, 2, 256], F32, "ut")
+            for cc in range(2):
+                ct = 2 * cp + cc
+                nc.tensor.matmul_mx(out=ut[:, cc, :], lhsT=w1c[:, 1, ct * P:(ct + 1) * P].bitcast(FP8X4),
+                                    lhsT_scale=w1s[:, 1, ct * P:(ct + 1) * P],
+                                    rhs=acf.bitcast(FP8X4), rhs_scale=ascf, start=True, stop=True)
+            for cc in range(2):
+                ct = 2 * cp + cc
+                wsb = work.tile([P, 256], F32, name="wsb")
+                nc.scalar.activation(out=wsb[:], in_=ut[:, cc, :], func=ACT.Identity, bias=b1[:, ct:ct + 1], scale=s1[:, ct:ct + 1])
+                nc.vector.scalar_tensor_tensor(out=fin[:, ct, :, :].rearrange("p g n -> p (g n)"),
+                                               in0=rm[:, ct, :, :].rearrange("p g n -> p (g n)"),
+                                               scalar=s1abs[:, ct:ct + 1], in1=wsb[:], op0=ALU.mult, op1=ALU.add)
+        for g in range(2):
+            o_ps = ps_b([P, 512], F32, "o_ps")
+            for ct in range(4):
+                nc.tensor.transpose(o_ps[:, ct * P:(ct + 1) * P], fin[:, ct, g, :], ident_f[:])
+            o_sb = work.tile([P, 512], F32, name="o_sb")
+            if g == 0:
+                nc.scalar.activation(out=o_sb[:], in_=o_ps[:], func=ACT.Relu)
+            else:
+                nc.vector.tensor_scalar(out=o_sb[:], in0=o_ps[:], scalar1=0.0, scalar2=None, op0=ALU.max)
+            nc.sync.dma_start(out=out[g * P:(g + 1) * P, :], in_=o_sb[:])

@@ -23,9 +23,14 @@ BPG = 16
 FLOPS = 2 * (ROWS * 128 * 512 + ROWS * 512 * 512 + NVOX * 512 * 512)
 
 
+def on_vector(k, t):
+    return k < 2 and t % 2 == 1
+
+
 def tile_vfe_t_kernel(tc, voxel_feats, W0, gamma0, beta0, W1, gamma1, beta1, out):
     nc = tc.nc
     with ExitStack() as ctx:
+        ctx.enter_context(tc.manual_schedule())
         keep = ctx.enter_context(tc.tile_pool(name="keep", bufs=1))
         work = ctx.enter_context(tc.tile_pool(name="work", bufs=3))
         psum = ctx.enter_context(tc.psum_pool(name="psum", bufs=1))
@@ -68,9 +73,11 @@ def tile_vfe_t_kernel(tc, voxel_feats, W0, gamma0, beta0, W1, gamma1, beta1, out
         make_identity(nc, ident_bf[:])
         ident_f = keep.tile([P, P], F32, name="ident_f")
         make_identity(nc, ident_f[:])
-        pick = keep.tile([P, 2], F32, name="pick")
+        pick = keep.tile([P, 3, 2], F32, name="pick")
         nc.vector.memset(pick[:], 0.0)
-        nc.vector.memset(pick[:, 0:1], 1.0)
+        nc.vector.memset(pick[:, 0, 0:1], 1.0)
+        nc.vector.memset(pick[:, 1, 0:1], 2.0)
+        nc.vector.memset(pick[:, 2, 0:1], float(NPTS))
         gs = keep.tile([P, 130], F32, name="gs")
         nc.vector.memset(gs[:, 128:130], 0.0)
 
@@ -117,23 +124,6 @@ def tile_vfe_t_kernel(tc, voxel_feats, W0, gamma0, beta0, W1, gamma1, beta1, out
                 nc.vector.tensor_scalar(out=xt[:, b, :], in0=flat, scalar1=1.0, scalar2=None, op0=ALU.mult,
                                         op1=ALU.add, accum_out=sx_v[:, b // 2:b // 2 + 1])
 
-        w1w = w1_sb[:].bitcast(F32)
-        w1g = keep.tile([P, 2, 512, 4], BF16, name="w1g", align_bytes=64)
-        w1gw = w1g[:].bitcast(F32)
-        w1c = keep.tile([P, 2, 512], U32, name="w1c", align_bytes=64)
-        w1s = keep.tile([P, 2, 512], U8, name="w1s", align_bytes=64)
-        for h in range(2):
-            for cp in range(2):
-                wt_ps = ps_a([P, 2, 2, P], F32, "wt_ps")
-                for u in range(2):
-                    for cc in range(2):
-                        nc.tensor.transpose(wt_ps[:, u, cc, :], w1w[:, 2 * cp + cc, 256 * h + u:256 * h + 256:2], ident_f[:])
-                nc.vector.tensor_copy(out=w1gw[:, h, 256 * cp:256 * (cp + 1), :],
-                                      in_=wt_ps[:].rearrange("p u c i -> p (c i) u"))
-        for h in range(2):
-            nc.vector.quantize_mx(out=w1c[:, h, :].bitcast(FP8X4), scales=w1s[:, h, :],
-                                  in_=w1g[:, h, :, :].rearrange("p c t -> p (c t)"))
-
         nc.vector.tensor_copy(out=gs[:, 0:128], in_=g_ps[:])
         sxa = keep.tile([P, 1], F32, name="sxa")
         nc.vector.tensor_reduce(out=sxa[:], in_=sx_s[:], axis=AX.X, op=ALU.add)
@@ -142,10 +132,37 @@ def tile_vfe_t_kernel(tc, voxel_feats, W0, gamma0, beta0, W1, gamma1, beta1, out
         nc.vector.tensor_tensor(out=gs[:, 128:129], in0=sxa[:], in1=sxb[:], op=ALU.add)
         prod = keep.tile([P, 4, P], F32, name="prod")
         mean0 = keep.tile([P, 4], F32, name="mean0")
+        tqs = []
         for h in range(2):
             tq = ps_a([P, 2, 130], F32, "tq")
+            tqs.append(tq)
             for tt in range(2):
                 nc.tensor.matmul(tq[:, tt, :], lhsT=w0t_f[:, 2 * h + tt, :], rhs=gs[:], start=True, stop=True)
+
+        w1w = w1_sb[:].bitcast(F32)
+        w1g = keep.tile([P, 2, 512, 4], BF16, name="w1g", align_bytes=64)
+        w1gw = w1g[:].bitcast(F32)
+        w1c = keep.tile([P, 2, 512], U32, name="w1c", align_bytes=64)
+        w1s = keep.tile([P, 2, 512], U8, name="w1s", align_bytes=64)
+        wts = {}
+        for h in range(2):
+            for cp in range(2):
+                wt_ps = ps_b([P, 2, 2, P], F32, "wt_ps")
+                wts[(h, cp)] = wt_ps
+                for u in range(2):
+                    for cc in range(2):
+                        nc.tensor.transpose(wt_ps[:, u, cc, :], w1w[:, 2 * cp + cc, 256 * h + u:256 * h + 256:2], ident_f[:])
+
+        def w1_copy(h, cp):
+            nc.scalar.copy(out=w1gw[:, h, 256 * cp:256 * (cp + 1), :], in_=wts[(h, cp)][:].rearrange("p u c i -> p (c i) u"))
+
+        def w1_quantise(h):
+            nc.vector.quantize_mx(out=w1c[:, h, :].bitcast(FP8X4), scales=w1s[:, h, :],
+                                  in_=w1g[:, h, :, :].rearrange("p c t -> p (c t)"))
+
+        w1_copy(0, 0)
+        for h in range(2):
+            tq = tqs[h]
             nc.vector.tensor_tensor(out=prod[:, 2 * h:2 * h + 2, :], in0=tq[:, :, 0:128], in1=w0_f[:, 2 * h:2 * h + 2, :], op=ALU.mult)
             nc.vector.tensor_scalar(out=mean0[:, 2 * h:2 * h + 2], in0=tq[:, :, 128], scalar1=1.0 / ROWS, scalar2=None, op0=ALU.mult)
         q0 = keep.tile([P, 4], F32, name="q0")
@@ -170,6 +187,7 @@ def tile_vfe_t_kernel(tc, voxel_feats, W0, gamma0, beta0, W1, gamma1, beta1, out
             return scl, sft
 
         s0, b0 = scale_and_shift(q0[:], mean0[:], g0[:], be0[:], "0")
+        w1_copy(0, 1)
 
         ssq = keep.tile([P, 4, NBLK], F32, name="ssq")
         rmax = [[keep.tile([P, 512], F32, name="rmax%d%d" % (g, ct)) for ct in range(4)] for g in range(2)]
@@ -178,105 +196,222 @@ def tile_vfe_t_kernel(tc, voxel_feats, W0, gamma0, beta0, W1, gamma1, beta1, out
         agr = keep.tile([P, 2, 512], BF16, name="agr", align_bytes=64)
         ac = keep.tile([P, 2, P], U32, name="ac", align_bytes=64)
         asc = keep.tile([P, 2, P], U8, name="asc", align_bytes=64)
-        e1 = [keep.tile([P, 512], F32, name="e1_%d" % g) for g in range(2)]
-        e2 = [keep.tile([P, 512], F32, name="e2_%d" % g) for g in range(2)]
-        prev_gr = None
-        zs_ps = None
-        for b in range(NBLK):
-            g, mb = divmod(b, BPG)
-            pt = work.tile([P, 4, 512], BF16, name="pt")
-            for t in range(4):
-                y0 = ps_a([P, 512], F32, "y0")
-                nc.tensor.matmul(y0[:], lhsT=w0t[:, t, :], rhs=xt[:, b, :], start=True, stop=True)
-                nc.scalar.activation(out=pt[:, t, :], in_=y0[:], func=ACT.Relu, bias=b0[:, t:t + 1], scale=s0[:, t:t + 1])
+        zs_sb = [keep.tile([P, 512], F32, name="zs_sb%d" % g) for g in range(2)]
+        u_sb = [keep.tile([P, 512], F32, name="u_sb%d" % g) for g in range(2)]
+        uu = [keep.tile([P, 512], F32, name="uu%d" % g) for g in range(2)]
+        uz = [keep.tile([P, 512], F32, name="uz%d" % g) for g in range(2)]
+        st0 = keep.tile([P, 2, 4], F32, name="st0")
+        y0s = {}
+        pts = {}
+        grs = {}
+        cds = {}
+        zts = {}
+        zsum = {}
+        ups = {}
+
+        def l0(k, t):
+            y0 = ps_a([P, 512], F32, "y0")
+            y0s[(k, t)] = y0
+            nc.tensor.matmul(y0[:], lhsT=w0t[:, t, :], rhs=xt[:, k, :], start=True, stop=True)
+
+        def affine(k, t):
+            if t == 0:
+                pts[k] = work.tile([P, 4, 512], BF16, name="pt")
+            if on_vector(k, t):
+                nc.vector.tensor_scalar(out=pts[k][:, t, :], in0=y0s[(k, t)][:], scalar1=s0[:, t:t + 1],
+                                        scalar2=b0[:, t:t + 1], op0=ALU.mult, op1=ALU.add)
+            else:
+                nc.scalar.activation(out=pts[k][:, t, :], in_=y0s[(k, t)][:], func=ACT.Relu,
+                                     bias=b0[:, t:t + 1], scale=s0[:, t:t + 1])
+
+        def layer0(k):
+            for t in range(3):
+                l0(k, t)
+            affine(k, 0)
+            l0(k, 3)
+            for t in range(1, 4):
+                affine(k, t)
+
+        def regroup(k, engine):
             gr = work.tile([P, 512, 4], BF16, name="gr", align_bytes=64)
-            nc.vector.tensor_copy(out=gr[:].rearrange("p (c i) t -> p c t i", i=4),
-                                  in_=pt[:].rearrange("p t (c i) -> p c t i", i=4))
-            grf = gr[:].rearrange("p r t -> p (r t)")
+            grs[k] = gr
+            if engine == "vector":
+                nc.vector.tensor_scalar(out=gr[:].rearrange("p (c i) t -> p c t i", i=4),
+                                        in0=pts[k][:].rearrange("p t (c i) -> p c t i", i=4),
+                                        scalar1=0.0, scalar2=None, op0=ALU.max)
+            else:
+                nc.gpsimd.tensor_scalar(out=gr[:], in0=pts[k][:].rearrange("p t r -> p r t"),
+                                        scalar1=1.0, scalar2=0.0, op0=ALU.mult, op1=ALU.add)
+
+        def flat_gr(k):
+            return grs[k][:].rearrange("p r t -> p (r t)")
+
+        def quantise(k):
             codes = work.tile([P, 512], U32, name="codes", align_bytes=64)
             scales = work.tile([P, 512], U8, name="scales", align_bytes=64)
-            nc.vector.quantize_mx(out=codes[:].bitcast(FP8X4), scales=scales[:], in_=grf)
+            cds[k] = (codes, scales)
+            nc.vector.quantize_mx(out=codes[:].bitcast(FP8X4), scales=scales[:], in_=flat_gr(k))
+
+        def amax(k):
+            g, mb = divmod(k, BPG)
             arf = arun[g][:].rearrange("p a r -> p (a r)")
             if mb == 1:
-                nc.vector.tensor_tensor(out=arf, in0=prev_gr, in1=grf, op=ALU.max)
+                nc.vector.tensor_tensor(out=arf, in0=flat_gr(k - 1), in1=flat_gr(k), op=ALU.max)
             elif mb > 1:
-                nc.vector.tensor_tensor(out=arf, in0=arf, in1=grf, op=ALU.max)
-            prev_gr = grf
+                nc.vector.tensor_tensor(out=arf, in0=arf, in1=flat_gr(k), op=ALU.max)
 
+        def z_passes(k):
+            codes, scales = cds[k]
             for ct in range(4):
                 z = ps_b([P, 512], F32, "z")
+                zts[(k, ct)] = z
                 nc.tensor.matmul_mx(out=z[:], lhsT=w1c[:, 0, ct * P:(ct + 1) * P].bitcast(FP8X4),
                                     lhsT_scale=w1s[:, 0, ct * P:(ct + 1) * P],
                                     rhs=codes[:].bitcast(FP8X4), rhs_scale=scales[:], start=True, stop=True)
+
+        def zsum_passes(k):
+            g, mb = divmod(k, BPG)
+            codes, scales = cds[k]
+            if mb == 0:
+                zsum[g] = ps_c([P, 512], F32, "zs_ps")
+            for mi in range(4):
+                nc.tensor.matmul_mx(out=zsum[g][:], lhsT=codes[:, mi * P:(mi + 1) * P].bitcast(FP8X4),
+                                    lhsT_scale=scales[:, mi * P:(mi + 1) * P],
+                                    rhs=w1c[:, 0, :].bitcast(FP8X4), rhs_scale=w1s[:, 0, :],
+                                    start=(mb == 0 and mi == 0), stop=(mb == BPG - 1 and mi == 3))
+
+        def squares(k):
+            for ct in range(4):
                 junk = work.tile([P, 512], BF16, name="junk")
-                nc.scalar.activation(out=junk[:], in_=z[:], func=ACT.Square, accum_out=ssq[:, ct, b:b + 1])
+                nc.scalar.activation(out=junk[:], in_=zts[(k, ct)][:], func=ACT.Square, accum_out=ssq[:, ct, k:k + 1])
+
+        def maxes(k):
+            g, mb = divmod(k, BPG)
+            for ct in range(4):
+                z = zts[(k, ct)]
                 if mb == 0:
                     nc.vector.tensor_scalar(out=rmax[g][ct][:], in0=z[:], scalar1=sgn[:, ct:ct + 1], scalar2=None, op0=ALU.mult)
                 else:
                     nc.vector.scalar_tensor_tensor(out=rmax[g][ct][:], in0=z[:], scalar=sgn[:, ct:ct + 1],
                                                    in1=rmax[g][ct][:], op0=ALU.mult, op1=ALU.max)
-            if mb == 0:
-                zs_ps = ps_c([P, 512], F32, "zs_ps")
-            for mi in range(4):
-                nc.tensor.matmul_mx(out=zs_ps[:], lhsT=codes[:, mi * P:(mi + 1) * P].bitcast(FP8X4),
-                                    lhsT_scale=scales[:, mi * P:(mi + 1) * P],
-                                    rhs=w1c[:, 0, :].bitcast(FP8X4), rhs_scale=w1s[:, 0, :],
-                                    start=(mb == 0 and mi == 0), stop=(mb == BPG - 1 and mi == 3))
 
-            if mb == BPG - 1:
-                zs = work.tile([P, 512], F32, name="zs")
-                nc.vector.tensor_copy(out=zs[:], in_=zs_ps[:])
-                a1 = work.tile([P, 2, 512], BF16, name="a1")
-                nc.vector.tensor_tensor(out=a1[:], in0=arun[g][:, 0:2, :], in1=arun[g][:, 2:4, :], op=ALU.max)
-                nc.vector.tensor_tensor(out=agr[:, g, :], in0=a1[:, 0, :], in1=a1[:, 1, :], op=ALU.max)
-                nc.vector.quantize_mx(out=ac[:, g, :].bitcast(FP8X4), scales=asc[:, g, :], in_=agr[:, g, :])
-                u_ps = ps_a([P, 512], F32, "u_ps")
-                nc.tensor.matmul_mx(out=u_ps[:], lhsT=ac[:, g, :].bitcast(FP8X4), lhsT_scale=asc[:, g, :],
-                                    rhs=w1c[:, 1, :].bitcast(FP8X4), rhs_scale=w1s[:, 1, :], start=True, stop=True)
-                nc.vector.scalar_tensor_tensor(out=e1[g][:], in0=u_ps[:], scalar=float(NPTS), in1=zs[:], op0=ALU.mult, op1=ALU.add)
-                t2 = work.tile([P, 512], F32, name="t2")
-                nc.vector.tensor_tensor(out=t2[:], in0=e1[g][:], in1=zs[:], op=ALU.add)
-                nc.vector.tensor_tensor(out=e2[g][:], in0=u_ps[:], in1=t2[:], op=ALU.mult)
-                for ct in range(4):
-                    nc.vector.tensor_reduce(out=rm[:, ct, g, :], in_=rmax[g][ct][:].rearrange("p (a n) -> p n a", a=4),
-                                            axis=AX.X, op=ALU.max)
+        def group_a(g):
+            a1 = work.tile([P, 2, 512], BF16, name="a1")
+            nc.vector.tensor_tensor(out=a1[:], in0=arun[g][:, 0:2, :], in1=arun[g][:, 2:4, :], op=ALU.max)
+            nc.vector.tensor_tensor(out=agr[:, g, :], in0=a1[:, 0, :], in1=a1[:, 1, :], op=ALU.max)
+            nc.vector.quantize_mx(out=ac[:, g, :].bitcast(FP8X4), scales=asc[:, g, :], in_=agr[:, g, :])
 
-        sum_ps = ps_a([P, 2, 4, 2, 2], F32, "sum_ps")
-        for g in range(2):
-            for qi in range(2):
-                src = e1[g] if qi == 0 else e2[g]
-                for ct in range(4):
-                    nc.tensor.matmul(sum_ps[:, qi, ct, g, :], lhsT=src[:, ct * P:(ct + 1) * P], rhs=pick[:], start=True, stop=True)
-        st = keep.tile([P, 2, 4], F32, name="st")
-        nc.vector.tensor_reduce(out=st[:].rearrange("p q c -> p (q c)"), in_=sum_ps[:].rearrange("p q c g k -> p (q c) (g k)"),
-                                axis=AX.X, op=ALU.add)
+        def group_zs_copy(g):
+            nc.scalar.copy(out=zs_sb[g][:], in_=zsum[g][:])
+
+        def group_u(g):
+            ups[g] = ps_c([P, 512], F32, "u_ps") if g == 0 else ps_a([P, 512], F32, "u_ps")
+            nc.tensor.matmul_mx(out=ups[g][:], lhsT=ac[:, g, :].bitcast(FP8X4), lhsT_scale=asc[:, g, :],
+                                rhs=w1c[:, 1, :].bitcast(FP8X4), rhs_scale=w1s[:, 1, :], start=True, stop=True)
+
+        def group_u_copy(g):
+            nc.scalar.copy(out=u_sb[g][:], in_=ups[g][:])
+
+        def group_uu(g):
+            nc.gpsimd.tensor_tensor(out=uu[g][:], in0=u_sb[g][:], in1=u_sb[g][:], op=ALU.mult)
+
+        def group_uz(g):
+            nc.gpsimd.tensor_tensor(out=uz[g][:], in0=u_sb[g][:], in1=zs_sb[g][:], op=ALU.mult)
+
+        def group_sums(sum_ps, g):
+            for ct in range(4):
+                cols = slice(ct * P, (ct + 1) * P)
+                nc.tensor.matmul(sum_ps[:, g, 0, ct, :], lhsT=zs_sb[g][:, cols], rhs=pick[:, 0, :], start=True, stop=False)
+                nc.tensor.matmul(sum_ps[:, g, 0, ct, :], lhsT=u_sb[g][:, cols], rhs=pick[:, 2, :], start=False, stop=True)
+                nc.tensor.matmul(sum_ps[:, g, 1, ct, :], lhsT=uz[g][:, cols], rhs=pick[:, 1, :], start=True, stop=False)
+                nc.tensor.matmul(sum_ps[:, g, 1, ct, :], lhsT=uu[g][:, cols], rhs=pick[:, 2, :], start=False, stop=True)
+
+        def group_rm(g, ct):
+            nc.vector.tensor_reduce(out=rm[:, ct, g, :], in_=rmax[g][ct][:].rearrange("p (a n) -> p n a", a=4),
+                                    axis=AX.X, op=ALU.max)
+
+        layer0(0)
+        regroup(0, "vector")
+        w1_quantise(0)
+        layer0(1)
+        nc.vector.tensor_scalar(out=pts[1][:, 1:4:2, :], in0=pts[1][:, 1:4:2, :], scalar1=0.0, scalar2=None, op0=ALU.max)
+        w1_copy(1, 0)
+        w1_copy(1, 1)
+
+        uts = []
+        for j in range(NBLK):
+            g, mb = divmod(j, BPG)
+            last = mb == BPG - 1
+            if j + 1 < NBLK:
+                regroup(j + 1, "gpsimd")
+            if j == BPG:
+                group_uu(0)
+            if j == BPG + 1:
+                group_uz(0)
+            quantise(j)
+            amax(j)
+            if j == 1:
+                w1_quantise(1)
+            if last:
+                group_a(g)
+            z_passes(j)
+            if j + 2 < NBLK:
+                for t in range(3):
+                    l0(j + 2, t)
+            zsum_passes(j)
+            squares(j)
+            if last:
+                group_zs_copy(g)
+                group_u(g)
+            if j == NBLK - 1:
+                acf = ac[:].rearrange("p g n -> p (g n)")
+                ascf = asc[:].rearrange("p g n -> p (g n)")
+                for cp in range(2):
+                    ut = ps_a([P, 2, 256], F32, "ut")
+                    uts.append(ut)
+                    for cc in range(2):
+                        ct = 2 * cp + cc
+                        nc.tensor.matmul_mx(out=ut[:, cc, :], lhsT=w1c[:, 1, ct * P:(ct + 1) * P].bitcast(FP8X4),
+                                            lhsT_scale=w1s[:, 1, ct * P:(ct + 1) * P],
+                                            rhs=acf.bitcast(FP8X4), rhs_scale=ascf, start=True, stop=True)
+            maxes(j)
+            if BPG <= j < BPG + 4:
+                group_rm(0, j - BPG)
+            if j + 2 < NBLK:
+                affine(j + 2, 0)
+                l0(j + 2, 3)
+                for t in range(1, 4):
+                    affine(j + 2, t)
+            if last:
+                group_u_copy(g)
+
+        group_uz(1)
+        group_uu(1)
+        sum_ps = ps_a([P, 2, 2, 4, 2], F32, "sum_ps")
+        group_sums(sum_ps, 0)
+        for ct in range(4):
+            group_rm(1, ct)
+        nc.vector.tensor_copy(out=st0[:], in_=sum_ps[:, 0, :, :, 0])
         ssqt = keep.tile([P, 4], F32, name="ssqt")
         nc.vector.tensor_reduce(out=ssqt[:], in_=ssq[:], axis=AX.X, op=ALU.add)
+        group_sums(sum_ps, 1)
+        stt = keep.tile([P, 2, 4], F32, name="stt")
+        nc.vector.tensor_tensor(out=stt[:], in0=sum_ps[:, 1, :, :, 0], in1=st0[:], op=ALU.add)
         q1 = keep.tile([P, 4], F32, name="q1")
-        nc.vector.tensor_tensor(out=q1[:], in0=ssqt[:], in1=st[:, 1, :], op=ALU.add)
+        nc.vector.tensor_tensor(out=q1[:], in0=ssqt[:], in1=stt[:, 1, :], op=ALU.add)
         mean1 = keep.tile([P, 4], F32, name="mean1")
-        nc.vector.tensor_scalar(out=mean1[:], in0=st[:, 0, :], scalar1=1.0 / ROWS, scalar2=None, op0=ALU.mult)
+        nc.vector.tensor_scalar(out=mean1[:], in0=stt[:, 0, :], scalar1=1.0 / ROWS, scalar2=None, op0=ALU.mult)
         s1, b1 = scale_and_shift(q1[:], mean1[:], gb1[:, 0:4], gb1[:, 4:8], "1")
         s1abs = keep.tile([P, 4], F32, name="s1abs")
         nc.vector.tensor_tensor(out=s1abs[:], in0=s1[:], in1=sgn[:], op=ALU.mult)
 
-        acf = ac[:].rearrange("p g n -> p (g n)")
-        ascf = asc[:].rearrange("p g n -> p (g n)")
         fin = keep.tile([P, 4, 2, P], F32, name="fin")
-        for cp in range(2):
-            ut = ps_b([P, 2, 256], F32, "ut")
-            for cc in range(2):
-                ct = 2 * cp + cc
-                nc.tensor.matmul_mx(out=ut[:, cc, :], lhsT=w1c[:, 1, ct * P:(ct + 1) * P].bitcast(FP8X4),
-                                    lhsT_scale=w1s[:, 1, ct * P:(ct + 1) * P],
-                                    rhs=acf.bitcast(FP8X4), rhs_scale=ascf, start=True, stop=True)
-            for cc in range(2):
-                ct = 2 * cp + cc
-                wsb = work.tile([P, 256], F32, name="wsb")
-                nc.scalar.activation(out=wsb[:], in_=ut[:, cc, :], func=ACT.Identity, bias=b1[:, ct:ct + 1], scale=s1[:, ct:ct + 1])
-                nc.vector.scalar_tensor_tensor(out=fin[:, ct, :, :].rearrange("p g n -> p (g n)"),
-                                               in0=rm[:, ct, :, :].rearrange("p g n -> p (g n)"),
-                                               scalar=s1abs[:, ct:ct + 1], in1=wsb[:], op0=ALU.mult, op1=ALU.add)
+        for ct in range(4):
+            wsb = work.tile([P, 256], F32, name="wsb")
+            nc.scalar.activation(out=wsb[:], in_=uts[ct // 2][:, ct % 2, :], func=ACT.Identity, bias=b1[:, ct:ct + 1], scale=s1[:, ct:ct + 1])
+            nc.vector.scalar_tensor_tensor(out=fin[:, ct, :, :].rearrange("p g n -> p (g n)"),
+                                           in0=rm[:, ct, :, :].rearrange("p g n -> p (g n)"),
+                                           scalar=s1abs[:, ct:ct + 1], in1=wsb[:], op0=ALU.mult, op1=ALU.add)
         for g in range(2):
             o_ps = ps_b([P, 512], F32, "o_ps")
             for ct in range(4):

@@ -20,11 +20,9 @@ EPS = 1e-3
 NBLK = 32
 BPG = 16
 
+CHUNKS = [(0, 0, 8), (0, 8, 8), (0, 16, 16), (0, 32, 16), (0, 48, 16), (1, 0, 16), (1, 16, 16), (1, 32, 16), (1, 48, 8), (1, 56, 8)]
+
 FLOPS = 2 * (ROWS * 128 * 512 + ROWS * 512 * 512 + NVOX * 512 * 512)
-
-
-def on_vector(k, t):
-    return k < 2 and t % 2 == 1
 
 
 def tile_vfe_t_kernel(tc, voxel_feats, W0, gamma0, beta0, W1, gamma1, beta1, out):
@@ -39,16 +37,18 @@ def tile_vfe_t_kernel(tc, voxel_feats, W0, gamma0, beta0, W1, gamma1, beta1, out
             return psum.tile(shape, dtype, name=name, tag="a", bufs=3)
 
         def ps_b(shape, dtype, name):
-            return psum.tile(shape, dtype, name=name, tag="b", bufs=4)
+            return psum.tile(shape, dtype, name=name, tag="b", bufs=3)
 
         def ps_c(shape, dtype, name):
             return psum.tile(shape, dtype, name=name, tag="c", bufs=1)
 
+        def ps_d(shape, dtype, name):
+            return psum.tile(shape, dtype, name=name, tag="d", bufs=1)
+
         x_sb = keep.tile([P, 2, NPTS, 128], BF16, name="x_sb")
         xv = voxel_feats.rearrange("(g n) m c -> n g m c", g=2)
-        for g in range(2):
-            for q in range(4):
-                nc.sync.dma_start(out=x_sb[:, g, 16 * q:16 * (q + 1), :], in_=xv[:, g, 16 * q:16 * (q + 1), :])
+        for g, m0, cnt in CHUNKS:
+            nc.sync.dma_start(out=x_sb[:, g, m0:m0 + cnt, :], in_=xv[:, g, m0:m0 + cnt, :])
         w1_sb = keep.tile([P, 4, 1024], BF16, name="w1_sb")
         w1v = W1.rearrange("(ct i) k -> i ct k", ct=4)
         for hh in range(2):
@@ -73,71 +73,62 @@ def tile_vfe_t_kernel(tc, voxel_feats, W0, gamma0, beta0, W1, gamma1, beta1, out
         make_identity(nc, ident_bf[:])
         ident_f = keep.tile([P, P], F32, name="ident_f")
         make_identity(nc, ident_f[:])
-        pick = keep.tile([P, 3, 2], F32, name="pick")
-        nc.vector.memset(pick[:], 0.0)
-        nc.vector.memset(pick[:, 0, 0:1], 1.0)
-        nc.vector.memset(pick[:, 1, 0:1], 2.0)
-        nc.vector.memset(pick[:, 2, 0:1], float(NPTS))
-        gs = keep.tile([P, 130], F32, name="gs")
-        nc.vector.memset(gs[:, 128:130], 0.0)
+        x_aug = keep.tile([P, 2, NPTS, 130], BF16, name="x_aug")
+        nc.vector.memset(x_aug[:, :, :, 128:130], 1.0)
 
         w0t_ps = ps_a([P, 4, P], BF16, "w0t_ps")
         for t in range(4):
             nc.tensor.transpose(w0t_ps[:, t, :], w0_sb[:, t, :], ident_bf[:])
-        w0t = keep.tile([P, 4, P], BF16, name="w0t")
-        nc.vector.tensor_copy(out=w0t[:], in_=w0t_ps[:])
-        w0t_f = keep.tile([P, 4, P], F32, name="w0t_f")
-        nc.vector.tensor_copy(out=w0t_f[:], in_=w0t_ps[:])
-        w0_f = keep.tile([P, 4, P], F32, name="w0_f")
-        nc.vector.tensor_copy(out=w0_f[:], in_=w0_sb[:])
-        g0 = keep.tile([P, 4], F32, name="g0")
-        nc.vector.tensor_copy(out=g0[:], in_=g0_bf[:])
-        be0 = keep.tile([P, 4], F32, name="be0")
-        nc.vector.tensor_copy(out=be0[:], in_=b0_bf[:])
-
         gb1_ps = ps_a([P, P], BF16, "gb1_ps")
         nc.tensor.transpose(gb1_ps[:], gb1_rows[:], ident_bf[:])
+        w0t = keep.tile([P, 4, P], BF16, name="w0t")
+        w0t_f = keep.tile([P, 4, P], F32, name="w0t_f")
+        w0_f = keep.tile([P, 4, P], F32, name="w0_f")
+        g0 = keep.tile([P, 4], F32, name="g0")
+        be0 = keep.tile([P, 4], F32, name="be0")
         gb1 = keep.tile([P, 8], F32, name="gb1")
-        nc.vector.tensor_copy(out=gb1[:], in_=gb1_ps[:, 0:8])
         pos = keep.tile([P, 4], F32, name="pos")
-        nc.vector.tensor_scalar(out=pos[:], in0=gb1[:, 0:4], scalar1=0.0, scalar2=None, op0=ALU.is_gt)
         neg = keep.tile([P, 4], F32, name="neg")
-        nc.vector.tensor_scalar(out=neg[:], in0=gb1[:, 0:4], scalar1=0.0, scalar2=None, op0=ALU.is_lt)
         sgn = keep.tile([P, 4], F32, name="sgn")
-        nc.vector.tensor_tensor(out=sgn[:], in0=pos[:], in1=neg[:], op=ALU.subtract)
 
-        g_ps = ps_c([P, P], F32, "g_ps")
+        def small_work(step):
+            if step == 0:
+                nc.vector.tensor_copy(out=w0t[:], in_=w0t_ps[:])
+            elif step == 1:
+                nc.vector.tensor_copy(out=w0t_f[:], in_=w0t_ps[:])
+            elif step == 2:
+                nc.vector.tensor_copy(out=w0_f[:], in_=w0_sb[:])
+            elif step == 3:
+                nc.vector.tensor_copy(out=g0[:], in_=g0_bf[:])
+                nc.vector.tensor_copy(out=be0[:], in_=b0_bf[:])
+                nc.vector.tensor_copy(out=gb1[:], in_=gb1_ps[:, 0:8])
+            elif step == 4:
+                nc.vector.tensor_scalar(out=pos[:], in0=gb1[:, 0:4], scalar1=0.0, scalar2=None, op0=ALU.is_gt)
+                nc.vector.tensor_scalar(out=neg[:], in0=gb1[:, 0:4], scalar1=0.0, scalar2=None, op0=ALU.is_lt)
+                nc.vector.tensor_tensor(out=sgn[:], in0=pos[:], in1=neg[:], op=ALU.subtract)
+
+        g_ps = ps_c([P, 130], F32, "g_ps")
+        for step, (g, m0, cnt) in enumerate(CHUNKS):
+            nc.vector.tensor_copy(out=x_aug[:, g, m0:m0 + cnt, 0:128], in_=x_sb[:, g, m0:m0 + cnt, :])
+            small_work(step)
+            for m in range(m0, m0 + cnt):
+                nc.tensor.matmul(g_ps[:], lhsT=x_sb[:, g, m, :], rhs=x_aug[:, g, m, :],
+                                 start=(g == 0 and m == 0), stop=(g == 1 and m == NPTS - 1))
+
         xt = keep.tile([P, NBLK, 512], BF16, name="xt")
-        sx_s = keep.tile([P, BPG], F32, name="sx_s")
-        sx_v = keep.tile([P, BPG], F32, name="sx_v")
-        for b in range(NBLK):
-            g, mb = divmod(b, BPG)
-            xt_ps = ps_b([P, 4, P], BF16, "xt_ps")
-            for mi in range(4):
-                xm = x_sb[:, g, 4 * mb + mi, :]
-                nc.tensor.transpose(xt_ps[:, mi, :], xm, ident_bf[:])
-                nc.tensor.matmul(g_ps[:], lhsT=xm, rhs=xm, start=(b == 0 and mi == 0), stop=(b == NBLK - 1 and mi == 3))
-            flat = xt_ps[:].rearrange("p a r -> p (a r)")
-            if b % 2 == 0:
-                nc.scalar.activation(out=xt[:, b, :], in_=flat, func=ACT.Copy, accum_out=sx_s[:, b // 2:b // 2 + 1])
-            else:
-                nc.vector.tensor_scalar(out=xt[:, b, :], in0=flat, scalar1=1.0, scalar2=None, op0=ALU.mult,
-                                        op1=ALU.add, accum_out=sx_v[:, b // 2:b // 2 + 1])
+        xt_ps = ps_d([P, 2, 4, P], BF16, "xt_ps")
 
-        nc.vector.tensor_copy(out=gs[:, 0:128], in_=g_ps[:])
-        sxa = keep.tile([P, 1], F32, name="sxa")
-        nc.vector.tensor_reduce(out=sxa[:], in_=sx_s[:], axis=AX.X, op=ALU.add)
-        sxb = keep.tile([P, 1], F32, name="sxb")
-        nc.vector.tensor_reduce(out=sxb[:], in_=sx_v[:], axis=AX.X, op=ALU.add)
-        nc.vector.tensor_tensor(out=gs[:, 128:129], in0=sxa[:], in1=sxb[:], op=ALU.add)
-        prod = keep.tile([P, 4, P], F32, name="prod")
-        mean0 = keep.tile([P, 4], F32, name="mean0")
-        tqs = []
-        for h in range(2):
-            tq = ps_a([P, 2, 130], F32, "tq")
-            tqs.append(tq)
-            for tt in range(2):
-                nc.tensor.matmul(tq[:, tt, :], lhsT=w0t_f[:, 2 * h + tt, :], rhs=gs[:], start=True, stop=True)
+        def xt_transposes(k):
+            g, mb = divmod(k, BPG)
+            for mi in range(4):
+                nc.tensor.transpose(xt_ps[:, k % 2, mi, :], x_sb[:, g, 4 * mb + mi, :], ident_bf[:])
+
+        def xt_copy(k, engine):
+            flat = xt_ps[:, k % 2, :, :].rearrange("p a r -> p (a r)")
+            if engine == "scalar":
+                nc.scalar.copy(out=xt[:, k, :], in_=flat)
+            else:
+                nc.vector.tensor_copy(out=xt[:, k, :], in_=flat)
 
         w1w = w1_sb[:].bitcast(F32)
         w1g = keep.tile([P, 2, 512, 4], BF16, name="w1g", align_bytes=64)
@@ -145,13 +136,12 @@ def tile_vfe_t_kernel(tc, voxel_feats, W0, gamma0, beta0, W1, gamma1, beta1, out
         w1c = keep.tile([P, 2, 512], U32, name="w1c", align_bytes=64)
         w1s = keep.tile([P, 2, 512], U8, name="w1s", align_bytes=64)
         wts = {}
-        for h in range(2):
-            for cp in range(2):
-                wt_ps = ps_b([P, 2, 2, P], F32, "wt_ps")
-                wts[(h, cp)] = wt_ps
-                for u in range(2):
-                    for cc in range(2):
-                        nc.tensor.transpose(wt_ps[:, u, cc, :], w1w[:, 2 * cp + cc, 256 * h + u:256 * h + 256:2], ident_f[:])
+
+        def w1_transposes(h, cp):
+            wts[(h, cp)] = ps_b([P, 2, 2, P], F32, "wt_ps")
+            for u in range(2):
+                for cc in range(2):
+                    nc.tensor.transpose(wts[(h, cp)][:, u, cc, :], w1w[:, 2 * cp + cc, 256 * h + u:256 * h + 256:2], ident_f[:])
 
         def w1_copy(h, cp):
             nc.scalar.copy(out=w1gw[:, h, 256 * cp:256 * (cp + 1), :], in_=wts[(h, cp)][:].rearrange("p u c i -> p (c i) u"))
@@ -159,14 +149,6 @@ def tile_vfe_t_kernel(tc, voxel_feats, W0, gamma0, beta0, W1, gamma1, beta1, out
         def w1_quantise(h):
             nc.vector.quantize_mx(out=w1c[:, h, :].bitcast(FP8X4), scales=w1s[:, h, :],
                                   in_=w1g[:, h, :, :].rearrange("p c t -> p (c t)"))
-
-        w1_copy(0, 0)
-        for h in range(2):
-            tq = tqs[h]
-            nc.vector.tensor_tensor(out=prod[:, 2 * h:2 * h + 2, :], in0=tq[:, :, 0:128], in1=w0_f[:, 2 * h:2 * h + 2, :], op=ALU.mult)
-            nc.vector.tensor_scalar(out=mean0[:, 2 * h:2 * h + 2], in0=tq[:, :, 128], scalar1=1.0 / ROWS, scalar2=None, op0=ALU.mult)
-        q0 = keep.tile([P, 4], F32, name="q0")
-        nc.vector.tensor_reduce(out=q0[:], in_=prod[:], axis=AX.X, op=ALU.add)
 
         def scale_and_shift(sumsq, mean, gam, bet, label):
             msq = keep.tile([P, 4], F32, name="msq" + label)
@@ -186,8 +168,27 @@ def tile_vfe_t_kernel(tc, voxel_feats, W0, gamma0, beta0, W1, gamma1, beta1, out
             nc.vector.tensor_tensor(out=sft[:], in0=bet, in1=msc[:], op=ALU.subtract)
             return scl, sft
 
+        xt_transposes(0)
+        gs = keep.tile([P, 130], F32, name="gs")
+        nc.vector.tensor_copy(out=gs[:], in_=g_ps[:])
+        tqs = []
+        for h in range(2):
+            tq = ps_a([P, 2, 130], F32, "tq")
+            tqs.append(tq)
+            for tt in range(2):
+                nc.tensor.matmul(tq[:, tt, :], lhsT=w0t_f[:, 2 * h + tt, :], rhs=gs[:], start=True, stop=True)
+        xt_copy(0, "scalar")
+        xt_transposes(1)
+        xt_copy(1, "scalar")
+        q0 = keep.tile([P, 4], F32, name="q0")
+        mean0 = keep.tile([P, 4], F32, name="mean0")
+        for t in range(4):
+            junk_q = work.tile([P, P], F32, name="junk_q")
+            nc.vector.scalar_tensor_tensor(out=junk_q[:], in0=tqs[t // 2][:, t % 2, 0:128], scalar=1.0, in1=w0_f[:, t, :],
+                                           op0=ALU.mult, op1=ALU.mult, accum_out=q0[:, t:t + 1])
+        for h in range(2):
+            nc.vector.tensor_scalar(out=mean0[:, 2 * h:2 * h + 2], in0=tqs[h][:, :, 128], scalar1=1.0 / ROWS, scalar2=None, op0=ALU.mult)
         s0, b0 = scale_and_shift(q0[:], mean0[:], g0[:], be0[:], "0")
-        w1_copy(0, 1)
 
         ssq = keep.tile([P, 4, NBLK], F32, name="ssq")
         rmax = [[keep.tile([P, 512], F32, name="rmax%d%d" % (g, ct)) for ct in range(4)] for g in range(2)]
@@ -197,50 +198,39 @@ def tile_vfe_t_kernel(tc, voxel_feats, W0, gamma0, beta0, W1, gamma1, beta1, out
         ac = keep.tile([P, 2, P], U32, name="ac", align_bytes=64)
         asc = keep.tile([P, 2, P], U8, name="asc", align_bytes=64)
         zs_sb = [keep.tile([P, 512], F32, name="zs_sb%d" % g) for g in range(2)]
-        u_sb = [keep.tile([P, 512], F32, name="u_sb%d" % g) for g in range(2)]
-        uu = [keep.tile([P, 512], F32, name="uu%d" % g) for g in range(2)]
-        uz = [keep.tile([P, 512], F32, name="uz%d" % g) for g in range(2)]
-        st0 = keep.tile([P, 2, 4], F32, name="st0")
+        zst_sb = keep.tile([P, 4, 2, P], F32, name="zst_sb")
+        sacc = keep.tile([P, 4, 4], F32, name="sacc")
+        a3 = keep.tile([P, 4], F32, name="a3")
         y0s = {}
         pts = {}
         grs = {}
         cds = {}
         zts = {}
         zsum = {}
-        ups = {}
+        zstp = {}
 
         def l0(k, t):
-            y0 = ps_a([P, 512], F32, "y0")
-            y0s[(k, t)] = y0
-            nc.tensor.matmul(y0[:], lhsT=w0t[:, t, :], rhs=xt[:, k, :], start=True, stop=True)
+            y0s[(k, t)] = ps_a([P, 512], F32, "y0")
+            nc.tensor.matmul(y0s[(k, t)][:], lhsT=w0t[:, t, :], rhs=xt[:, k, :], start=True, stop=True)
 
         def affine(k, t):
             if t == 0:
                 pts[k] = work.tile([P, 4, 512], BF16, name="pt")
-            if on_vector(k, t):
+            if k == 0 and t % 2 == 1:
                 nc.vector.tensor_scalar(out=pts[k][:, t, :], in0=y0s[(k, t)][:], scalar1=s0[:, t:t + 1],
                                         scalar2=b0[:, t:t + 1], op0=ALU.mult, op1=ALU.add)
             else:
                 nc.scalar.activation(out=pts[k][:, t, :], in_=y0s[(k, t)][:], func=ACT.Relu,
                                      bias=b0[:, t:t + 1], scale=s0[:, t:t + 1])
 
-        def layer0(k):
-            for t in range(3):
-                l0(k, t)
-            affine(k, 0)
-            l0(k, 3)
-            for t in range(1, 4):
-                affine(k, t)
-
-        def regroup(k, engine):
-            gr = work.tile([P, 512, 4], BF16, name="gr", align_bytes=64)
-            grs[k] = gr
-            if engine == "vector":
-                nc.vector.tensor_scalar(out=gr[:].rearrange("p (c i) t -> p c t i", i=4),
+        def regroup(k):
+            grs[k] = work.tile([P, 512, 4], BF16, name="gr", align_bytes=64, bufs=1)
+            if k == 0:
+                nc.vector.tensor_scalar(out=grs[k][:].rearrange("p (c i) t -> p c t i", i=4),
                                         in0=pts[k][:].rearrange("p t (c i) -> p c t i", i=4),
                                         scalar1=0.0, scalar2=None, op0=ALU.max)
             else:
-                nc.gpsimd.tensor_scalar(out=gr[:], in0=pts[k][:].rearrange("p t r -> p r t"),
+                nc.gpsimd.tensor_scalar(out=grs[k][:], in0=pts[k][:].rearrange("p t r -> p r t"),
                                         scalar1=1.0, scalar2=0.0, op0=ALU.mult, op1=ALU.add)
 
         def flat_gr(k):
@@ -255,19 +245,17 @@ def tile_vfe_t_kernel(tc, voxel_feats, W0, gamma0, beta0, W1, gamma1, beta1, out
         def amax(k):
             g, mb = divmod(k, BPG)
             arf = arun[g][:].rearrange("p a r -> p (a r)")
-            if mb == 1:
-                nc.vector.tensor_tensor(out=arf, in0=flat_gr(k - 1), in1=flat_gr(k), op=ALU.max)
-            elif mb > 1:
+            if mb == 0:
+                nc.vector.tensor_copy(out=arf, in_=flat_gr(k))
+            else:
                 nc.vector.tensor_tensor(out=arf, in0=arf, in1=flat_gr(k), op=ALU.max)
 
-        def z_passes(k):
+        def z_pass(k, ct):
             codes, scales = cds[k]
-            for ct in range(4):
-                z = ps_b([P, 512], F32, "z")
-                zts[(k, ct)] = z
-                nc.tensor.matmul_mx(out=z[:], lhsT=w1c[:, 0, ct * P:(ct + 1) * P].bitcast(FP8X4),
-                                    lhsT_scale=w1s[:, 0, ct * P:(ct + 1) * P],
-                                    rhs=codes[:].bitcast(FP8X4), rhs_scale=scales[:], start=True, stop=True)
+            zts[(k, ct)] = ps_a([P, 512], F32, "z") if (k == NBLK - 1 and ct == 3) else ps_b([P, 512], F32, "z")
+            nc.tensor.matmul_mx(out=zts[(k, ct)][:], lhsT=w1c[:, 0, ct * P:(ct + 1) * P].bitcast(FP8X4),
+                                lhsT_scale=w1s[:, 0, ct * P:(ct + 1) * P],
+                                rhs=codes[:].bitcast(FP8X4), rhs_scale=scales[:], start=True, stop=True)
 
         def zsum_passes(k):
             g, mb = divmod(k, BPG)
@@ -280,20 +268,18 @@ def tile_vfe_t_kernel(tc, voxel_feats, W0, gamma0, beta0, W1, gamma1, beta1, out
                                     rhs=w1c[:, 0, :].bitcast(FP8X4), rhs_scale=w1s[:, 0, :],
                                     start=(mb == 0 and mi == 0), stop=(mb == BPG - 1 and mi == 3))
 
-        def squares(k):
-            for ct in range(4):
-                junk = work.tile([P, 512], BF16, name="junk")
-                nc.scalar.activation(out=junk[:], in_=zts[(k, ct)][:], func=ACT.Square, accum_out=ssq[:, ct, k:k + 1])
+        def square(k, ct):
+            junk = work.tile([P, 512], BF16, name="junk")
+            nc.scalar.activation(out=junk[:], in_=zts[(k, ct)][:], func=ACT.Square, accum_out=ssq[:, ct, k:k + 1])
 
-        def maxes(k):
+        def maxi(k, ct):
             g, mb = divmod(k, BPG)
-            for ct in range(4):
-                z = zts[(k, ct)]
-                if mb == 0:
-                    nc.vector.tensor_scalar(out=rmax[g][ct][:], in0=z[:], scalar1=sgn[:, ct:ct + 1], scalar2=None, op0=ALU.mult)
-                else:
-                    nc.vector.scalar_tensor_tensor(out=rmax[g][ct][:], in0=z[:], scalar=sgn[:, ct:ct + 1],
-                                                   in1=rmax[g][ct][:], op0=ALU.mult, op1=ALU.max)
+            z = zts[(k, ct)]
+            if mb == 0:
+                nc.vector.tensor_scalar(out=rmax[g][ct][:], in0=z[:], scalar1=sgn[:, ct:ct + 1], scalar2=None, op0=ALU.mult)
+            else:
+                nc.vector.scalar_tensor_tensor(out=rmax[g][ct][:], in0=z[:], scalar=sgn[:, ct:ct + 1],
+                                               in1=rmax[g][ct][:], op0=ALU.mult, op1=ALU.max)
 
         def group_a(g):
             a1 = work.tile([P, 2, 512], BF16, name="a1")
@@ -304,65 +290,72 @@ def tile_vfe_t_kernel(tc, voxel_feats, W0, gamma0, beta0, W1, gamma1, beta1, out
         def group_zs_copy(g):
             nc.scalar.copy(out=zs_sb[g][:], in_=zsum[g][:])
 
-        def group_u(g):
-            ups[g] = ps_c([P, 512], F32, "u_ps") if g == 0 else ps_a([P, 512], F32, "u_ps")
-            nc.tensor.matmul_mx(out=ups[g][:], lhsT=ac[:, g, :].bitcast(FP8X4), lhsT_scale=asc[:, g, :],
-                                rhs=w1c[:, 1, :].bitcast(FP8X4), rhs_scale=w1s[:, 1, :], start=True, stop=True)
-
-        def group_u_copy(g):
-            nc.scalar.copy(out=u_sb[g][:], in_=ups[g][:])
-
-        def group_uu(g):
-            nc.gpsimd.tensor_tensor(out=uu[g][:], in0=u_sb[g][:], in1=u_sb[g][:], op=ALU.mult)
-
-        def group_uz(g):
-            nc.gpsimd.tensor_tensor(out=uz[g][:], in0=u_sb[g][:], in1=zs_sb[g][:], op=ALU.mult)
-
-        def group_sums(sum_ps, g):
+        def group_zs_transposes(g):
+            zstp[g] = ps_d([P, 4, P], F32, "zst_ps")
             for ct in range(4):
-                cols = slice(ct * P, (ct + 1) * P)
-                nc.tensor.matmul(sum_ps[:, g, 0, ct, :], lhsT=zs_sb[g][:, cols], rhs=pick[:, 0, :], start=True, stop=False)
-                nc.tensor.matmul(sum_ps[:, g, 0, ct, :], lhsT=u_sb[g][:, cols], rhs=pick[:, 2, :], start=False, stop=True)
-                nc.tensor.matmul(sum_ps[:, g, 1, ct, :], lhsT=uz[g][:, cols], rhs=pick[:, 1, :], start=True, stop=False)
-                nc.tensor.matmul(sum_ps[:, g, 1, ct, :], lhsT=uu[g][:, cols], rhs=pick[:, 2, :], start=False, stop=True)
+                nc.tensor.transpose(zstp[g][:, ct, :], zs_sb[g][:, ct * P:(ct + 1) * P], ident_f[:])
+
+        def group_zs_sums(g):
+            for ct in range(4):
+                nc.scalar.activation(out=zst_sb[:, ct, g, :], in_=zstp[g][:, ct, :], func=ACT.Copy, accum_out=sacc[:, g, ct:ct + 1])
 
         def group_rm(g, ct):
             nc.vector.tensor_reduce(out=rm[:, ct, g, :], in_=rmax[g][ct][:].rearrange("p (a n) -> p n a", a=4),
                                     axis=AX.X, op=ALU.max)
 
-        layer0(0)
-        regroup(0, "vector")
+        l0(0, 0)
+        l0(0, 1)
+        xt_transposes(2)
+        xt_copy(2, "scalar")
+        l0(0, 2)
+        w1_transposes(0, 0)
+        w1_transposes(0, 1)
+        affine(0, 0)
+        l0(0, 3)
+        for t in range(1, 4):
+            affine(0, t)
+        regroup(0)
+        w1_copy(0, 0)
+        w1_copy(0, 1)
         w1_quantise(0)
-        layer0(1)
-        nc.vector.tensor_scalar(out=pts[1][:, 1:4:2, :], in0=pts[1][:, 1:4:2, :], scalar1=0.0, scalar2=None, op0=ALU.max)
+        for t in range(3):
+            l0(1, t)
+        affine(1, 0)
+        l0(1, 3)
+        for t in range(1, 4):
+            affine(1, t)
+        xt_transposes(3)
+        w1_transposes(1, 0)
         w1_copy(1, 0)
+        w1_transposes(1, 1)
         w1_copy(1, 1)
 
         uts = []
         for j in range(NBLK):
             g, mb = divmod(j, BPG)
             last = mb == BPG - 1
-            if j + 1 < NBLK:
-                regroup(j + 1, "gpsimd")
-            if j == BPG:
-                group_uu(0)
-            if j == BPG + 1:
-                group_uz(0)
+            ahead = j + 2 < NBLK
             quantise(j)
             amax(j)
+            if j + 1 < NBLK:
+                regroup(j + 1)
             if j == 1:
                 w1_quantise(1)
             if last:
                 group_a(g)
-            z_passes(j)
-            if j + 2 < NBLK:
+            for ct in range(3):
+                z_pass(j, ct)
+            if ahead:
                 for t in range(3):
                     l0(j + 2, t)
+            square(j, 0)
+            maxi(j, 0)
+            z_pass(j, 3)
             zsum_passes(j)
-            squares(j)
-            if last:
-                group_zs_copy(g)
-                group_u(g)
+            if j + 4 < NBLK:
+                xt_transposes(j + 4)
+            if j == NBLK - 3:
+                group_zs_transposes(0)
             if j == NBLK - 1:
                 acf = ac[:].rearrange("p g n -> p (g n)")
                 ascf = asc[:].rearrange("p g n -> p (g n)")
@@ -374,33 +367,52 @@ def tile_vfe_t_kernel(tc, voxel_feats, W0, gamma0, beta0, W1, gamma1, beta1, out
                         nc.tensor.matmul_mx(out=ut[:, cc, :], lhsT=w1c[:, 1, ct * P:(ct + 1) * P].bitcast(FP8X4),
                                             lhsT_scale=w1s[:, 1, ct * P:(ct + 1) * P],
                                             rhs=acf.bitcast(FP8X4), rhs_scale=ascf, start=True, stop=True)
-            maxes(j)
-            if BPG <= j < BPG + 4:
-                group_rm(0, j - BPG)
-            if j + 2 < NBLK:
+            for ct in range(1, 4):
+                square(j, ct)
+            if ahead:
                 affine(j + 2, 0)
                 l0(j + 2, 3)
+            if last:
+                group_zs_copy(g)
+            for ct in range(1, 4):
+                maxi(j, ct)
+            if j + 3 < NBLK:
+                xt_copy(j + 3, "vector")
+            if BPG <= j < BPG + 4:
+                group_rm(0, j - BPG)
+            if ahead:
                 for t in range(1, 4):
                     affine(j + 2, t)
-            if last:
-                group_u_copy(g)
+            if j == NBLK - 2:
+                group_zs_sums(0)
 
-        group_uz(1)
-        group_uu(1)
-        sum_ps = ps_a([P, 2, 2, 4, 2], F32, "sum_ps")
-        group_sums(sum_ps, 0)
+        group_zs_transposes(1)
+        group_zs_sums(1)
+        for ct in range(4):
+            u_ct = uts[ct // 2][:, ct % 2, :]
+            junk_a = work.tile([P, 256], BF16, name="junk_a")
+            nc.scalar.activation(out=junk_a[:], in_=u_ct, func=ACT.Copy, accum_out=sacc[:, 2, ct:ct + 1])
+            junk_b = work.tile([P, 256], BF16, name="junk_b")
+            nc.scalar.activation(out=junk_b[:], in_=u_ct, func=ACT.Square, accum_out=sacc[:, 3, ct:ct + 1])
         for ct in range(4):
             group_rm(1, ct)
-        nc.vector.tensor_copy(out=st0[:], in_=sum_ps[:, 0, :, :, 0])
+        for ct in range(4):
+            junk_c = work.tile([P, 256], F32, name="junk_c")
+            nc.vector.scalar_tensor_tensor(out=junk_c[:], in0=uts[ct // 2][:, ct % 2, :], scalar=1.0,
+                                           in1=zst_sb[:, ct, :, :].rearrange("p g n -> p (g n)"),
+                                           op0=ALU.mult, op1=ALU.mult, accum_out=a3[:, ct:ct + 1])
         ssqt = keep.tile([P, 4], F32, name="ssqt")
         nc.vector.tensor_reduce(out=ssqt[:], in_=ssq[:], axis=AX.X, op=ALU.add)
-        group_sums(sum_ps, 1)
-        stt = keep.tile([P, 2, 4], F32, name="stt")
-        nc.vector.tensor_tensor(out=stt[:], in0=sum_ps[:, 1, :, :, 0], in1=st0[:], op=ALU.add)
-        q1 = keep.tile([P, 4], F32, name="q1")
-        nc.vector.tensor_tensor(out=q1[:], in0=ssqt[:], in1=stt[:, 1, :], op=ALU.add)
+        lin0 = keep.tile([P, 4], F32, name="lin0")
+        nc.vector.tensor_tensor(out=lin0[:], in0=sacc[:, 0, :], in1=sacc[:, 1, :], op=ALU.add)
+        lin = keep.tile([P, 4], F32, name="lin")
+        nc.vector.scalar_tensor_tensor(out=lin[:], in0=sacc[:, 2, :], scalar=float(NPTS), in1=lin0[:], op0=ALU.mult, op1=ALU.add)
         mean1 = keep.tile([P, 4], F32, name="mean1")
-        nc.vector.tensor_scalar(out=mean1[:], in0=stt[:, 0, :], scalar1=1.0 / ROWS, scalar2=None, op0=ALU.mult)
+        nc.vector.tensor_scalar(out=mean1[:], in0=lin[:], scalar1=1.0 / ROWS, scalar2=None, op0=ALU.mult)
+        half = keep.tile([P, 4], F32, name="half")
+        nc.vector.scalar_tensor_tensor(out=half[:], in0=sacc[:, 3, :], scalar=0.5 * NPTS, in1=a3[:], op0=ALU.mult, op1=ALU.add)
+        q1 = keep.tile([P, 4], F32, name="q1")
+        nc.vector.scalar_tensor_tensor(out=q1[:], in0=half[:], scalar=2.0, in1=ssqt[:], op0=ALU.mult, op1=ALU.add)
         s1, b1 = scale_and_shift(q1[:], mean1[:], gb1[:, 0:4], gb1[:, 4:8], "1")
         s1abs = keep.tile([P, 4], F32, name="s1abs")
         nc.vector.tensor_tensor(out=s1abs[:], in0=s1[:], in1=sgn[:], op=ALU.mult)

@@ -34,10 +34,10 @@ def tile_vfe_t_kernel(tc, voxel_feats, W0, gamma0, beta0, W1, gamma1, beta1, out
         psum = ctx.enter_context(tc.psum_pool(name="psum", bufs=1))
 
         def ps_a(shape, dtype, name):
-            return psum.tile(shape, dtype, name=name, tag="a", bufs=3)
+            return psum.tile(shape, dtype, name=name, tag="a", bufs=2)
 
         def ps_b(shape, dtype, name):
-            return psum.tile(shape, dtype, name=name, tag="b", bufs=3)
+            return psum.tile(shape, dtype, name=name, tag="b", bufs=4)
 
         def ps_c(shape, dtype, name):
             return psum.tile(shape, dtype, name=name, tag="c", bufs=1)
@@ -144,7 +144,12 @@ def tile_vfe_t_kernel(tc, voxel_feats, W0, gamma0, beta0, W1, gamma1, beta1, out
                     nc.tensor.transpose(wts[(h, cp)][:, u, cc, :], w1w[:, 2 * cp + cc, 256 * h + u:256 * h + 256:2], ident_f[:])
 
         def w1_copy(h, cp):
-            nc.scalar.copy(out=w1gw[:, h, 256 * cp:256 * (cp + 1), :], in_=wts[(h, cp)][:].rearrange("p u c i -> p (c i) u"))
+            words = w1gw[:, h, 256 * cp:256 * (cp + 1), :]
+            planes = wts[(h, cp)][:].rearrange("p u c i -> p (c i) u")
+            if h == 0:
+                nc.scalar.copy(out=words, in_=planes)
+            else:
+                nc.vector.tensor_copy(out=words, in_=planes)
 
         def w1_quantise(h):
             nc.vector.quantize_mx(out=w1c[:, h, :].bitcast(FP8X4), scales=w1s[:, h, :],
@@ -180,6 +185,11 @@ def tile_vfe_t_kernel(tc, voxel_feats, W0, gamma0, beta0, W1, gamma1, beta1, out
         xt_copy(0, "scalar")
         xt_transposes(1)
         xt_copy(1, "scalar")
+        xt_transposes(2)
+        xt_copy(2, "scalar")
+        w1_transposes(0, 0)
+        w1_transposes(0, 1)
+        xt_transposes(3)
         q0 = keep.tile([P, 4], F32, name="q0")
         mean0 = keep.tile([P, 4], F32, name="mean0")
         for t in range(4):
@@ -189,6 +199,8 @@ def tile_vfe_t_kernel(tc, voxel_feats, W0, gamma0, beta0, W1, gamma1, beta1, out
         for h in range(2):
             nc.vector.tensor_scalar(out=mean0[:, 2 * h:2 * h + 2], in0=tqs[h][:, :, 128], scalar1=1.0 / ROWS, scalar2=None, op0=ALU.mult)
         s0, b0 = scale_and_shift(q0[:], mean0[:], g0[:], be0[:], "0")
+        w1_copy(0, 0)
+        w1_copy(0, 1)
 
         ssq = keep.tile([P, 4, NBLK], F32, name="ssq")
         rmax = [[keep.tile([P, 512], F32, name="rmax%d%d" % (g, ct)) for ct in range(4)] for g in range(2)]
@@ -210,7 +222,7 @@ def tile_vfe_t_kernel(tc, voxel_feats, W0, gamma0, beta0, W1, gamma1, beta1, out
         zstp = {}
 
         def l0(k, t):
-            y0s[(k, t)] = ps_a([P, 512], F32, "y0")
+            y0s[(k, t)] = ps_b([P, 512], F32, "y0") if (k < 3 and t < 2) else ps_a([P, 512], F32, "y0")
             nc.tensor.matmul(y0s[(k, t)][:], lhsT=w0t[:, t, :], rhs=xt[:, k, :], start=True, stop=True)
 
         def affine(k, t):
@@ -252,7 +264,7 @@ def tile_vfe_t_kernel(tc, voxel_feats, W0, gamma0, beta0, W1, gamma1, beta1, out
 
         def z_pass(k, ct):
             codes, scales = cds[k]
-            zts[(k, ct)] = ps_a([P, 512], F32, "z") if (k == NBLK - 1 and ct == 3) else ps_b([P, 512], F32, "z")
+            zts[(k, ct)] = ps_b([P, 512], F32, "z")
             nc.tensor.matmul_mx(out=zts[(k, ct)][:], lhsT=w1c[:, 0, ct * P:(ct + 1) * P].bitcast(FP8X4),
                                 lhsT_scale=w1s[:, 0, ct * P:(ct + 1) * P],
                                 rhs=codes[:].bitcast(FP8X4), rhs_scale=scales[:], start=True, stop=True)
@@ -303,91 +315,118 @@ def tile_vfe_t_kernel(tc, voxel_feats, W0, gamma0, beta0, W1, gamma1, beta1, out
             nc.vector.tensor_reduce(out=rm[:, ct, g, :], in_=rmax[g][ct][:].rearrange("p (a n) -> p n a", a=4),
                                     axis=AX.X, op=ALU.max)
 
-        l0(0, 0)
-        l0(0, 1)
-        xt_transposes(2)
-        xt_copy(2, "scalar")
-        l0(0, 2)
-        w1_transposes(0, 0)
-        w1_transposes(0, 1)
-        affine(0, 0)
-        l0(0, 3)
-        for t in range(1, 4):
-            affine(0, t)
-        regroup(0)
-        w1_copy(0, 0)
-        w1_copy(0, 1)
-        w1_quantise(0)
-        for t in range(3):
-            l0(1, t)
-        affine(1, 0)
-        l0(1, 3)
-        for t in range(1, 4):
-            affine(1, t)
-        xt_transposes(3)
-        w1_transposes(1, 0)
-        w1_copy(1, 0)
-        w1_transposes(1, 1)
-        w1_copy(1, 1)
-
         uts = []
-        for j in range(NBLK):
-            g, mb = divmod(j, BPG)
-            last = mb == BPG - 1
-            ahead = j + 2 < NBLK
-            quantise(j)
-            amax(j)
-            if j + 1 < NBLK:
-                regroup(j + 1)
-            if j == 1:
-                w1_quantise(1)
-            if last:
-                group_a(g)
-            for ct in range(3):
-                z_pass(j, ct)
-            if ahead:
-                for t in range(3):
-                    l0(j + 2, t)
-            square(j, 0)
-            maxi(j, 0)
-            z_pass(j, 3)
-            zsum_passes(j)
-            if j + 4 < NBLK:
-                xt_transposes(j + 4)
-            if j == NBLK - 3:
-                group_zs_transposes(0)
-            if j == NBLK - 1:
-                acf = ac[:].rearrange("p g n -> p (g n)")
-                ascf = asc[:].rearrange("p g n -> p (g n)")
-                for cp in range(2):
-                    ut = ps_a([P, 2, 256], F32, "ut")
-                    uts.append(ut)
-                    for cc in range(2):
-                        ct = 2 * cp + cc
-                        nc.tensor.matmul_mx(out=ut[:, cc, :], lhsT=w1c[:, 1, ct * P:(ct + 1) * P].bitcast(FP8X4),
-                                            lhsT_scale=w1s[:, 1, ct * P:(ct + 1) * P],
-                                            rhs=acf.bitcast(FP8X4), rhs_scale=ascf, start=True, stop=True)
-            for ct in range(1, 4):
-                square(j, ct)
-            if ahead:
-                affine(j + 2, 0)
-                l0(j + 2, 3)
-            if last:
-                group_zs_copy(g)
-            for ct in range(1, 4):
-                maxi(j, ct)
-            if j + 3 < NBLK:
-                xt_copy(j + 3, "vector")
-            if BPG <= j < BPG + 4:
-                group_rm(0, j - BPG)
-            if ahead:
-                for t in range(1, 4):
-                    affine(j + 2, t)
-            if j == NBLK - 2:
-                group_zs_sums(0)
 
-        group_zs_transposes(1)
-        group_zs_sums(1)
+        def u_passes():
+            acf = ac[:].rearrange("p g n -> p (g n)")
+            ascf = asc[:].rearrange("p g n -> p (g n)")
+            for cp in range(2):
+                ut = ps_a([P, 2, 256], F32, "ut")
+                uts.append(ut)
+                for cc in range(2):
+                    ct = 2 * cp + cc
+                    nc.tensor.matmul_mx(out=ut[:, cc, :], lhsT=w1c[:, 1, ct * P:(ct + 1) * P].bitcast(FP8X4),
+                                        lhsT_scale=w1s[:, 1, ct * P:(ct + 1) * P],
+                                        rhs=acf.bitcast(FP8X4), rhs_scale=ascf, start=True, stop=True)
+
+        def quantise_and_max(k):
+            quantise(k)
+            amax(k)
+            if k == 3:
+                w1_quantise(1)
+            if k % BPG == BPG - 1:
+                group_a(k // BPG)
+
+        def sums_over_points(k):
+            zsum_passes(k)
+            if k == NBLK - 3:
+                group_zs_transposes(0)
+            if k == NBLK - 1:
+                u_passes()
+
+        for t in range(4):
+            l0(0, t)
+        for t in range(4):
+            affine(0, t)
+        w1_quantise(0)
+        regroup(0)
+        quantise_and_max(0)
+        for t in range(4):
+            l0(1, t)
+        for t in range(4):
+            affine(1, t)
+        regroup(1)
+        w1_transposes(1, 0)
+        w1_transposes(1, 1)
+        xt_copy(3, "vector")
+        w1_copy(1, 0)
+        w1_copy(1, 1)
+        for t in range(4):
+            l0(2, t)
+        xt_transposes(4)
+        xt_copy(4, "vector")
+        z_pass(0, 0)
+        z_pass(0, 1)
+        sums_over_points(0)
+        for t in range(4):
+            affine(2, t)
+        l0(3, 0)
+        l0(3, 1)
+
+        def have(k):
+            return k < NBLK
+
+        for i in range(NBLK):
+            if have(i + 2):
+                regroup(i + 2)
+            if have(i + 1):
+                quantise_and_max(i + 1)
+            if have(i + 3):
+                affine(i + 3, 0)
+            square(i, 0)
+            z_pass(i, 2)
+            if have(i + 3):
+                l0(i + 3, 2)
+                affine(i + 3, 1)
+            square(i, 1)
+            z_pass(i, 3)
+            if have(i + 5):
+                xt_transposes(i + 5)
+            if have(i + 3):
+                l0(i + 3, 3)
+            if have(i + 1):
+                sums_over_points(i + 1)
+            maxi(i, 0)
+            if have(i + 3):
+                affine(i + 3, 2)
+            square(i, 2)
+            if have(i + 4):
+                l0(i + 4, 0)
+            if have(i + 1):
+                z_pass(i + 1, 0)
+            maxi(i, 1)
+            if have(i + 3):
+                affine(i + 3, 3)
+            square(i, 3)
+            if i == BPG - 2:
+                group_zs_copy(0)
+            if i == NBLK - 3:
+                group_zs_sums(0)
+            if i == NBLK - 2:
+                group_zs_copy(1)
+                group_zs_transposes(1)
+                group_zs_sums(1)
+            if have(i + 4):
+                l0(i + 4, 1)
+            if have(i + 1):
+                z_pass(i + 1, 1)
+            maxi(i, 2)
+            if have(i + 5):
+                xt_copy(i + 5, "vector")
+            maxi(i, 3)
+            if BPG <= i < BPG + 4:
+                group_rm(0, i - BPG)
+
         for ct in range(4):
             u_ct = uts[ct // 2][:, ct % 2, :]
             junk_a = work.tile([P, 256], BF16, name="junk_a")

@@ -138,18 +138,13 @@ def tile_vfe_t_kernel(tc, voxel_feats, W0, gamma0, beta0, W1, gamma1, beta1, out
         wts = {}
 
         def w1_transposes(h, cp):
-            wts[(h, cp)] = ps_b([P, 2, 2, P], F32, "wt_ps")
+            wts[(h, cp)] = ps_b([P, 2, 2, P], F32, "wt_ps") if h == 0 else ps_a([P, 2, 2, P], F32, "wt_ps")
             for u in range(2):
                 for cc in range(2):
                     nc.tensor.transpose(wts[(h, cp)][:, u, cc, :], w1w[:, 2 * cp + cc, 256 * h + u:256 * h + 256:2], ident_f[:])
 
         def w1_copy(h, cp):
-            words = w1gw[:, h, 256 * cp:256 * (cp + 1), :]
-            planes = wts[(h, cp)][:].rearrange("p u c i -> p (c i) u")
-            if h == 0:
-                nc.scalar.copy(out=words, in_=planes)
-            else:
-                nc.vector.tensor_copy(out=words, in_=planes)
+            nc.scalar.copy(out=w1gw[:, h, 256 * cp:256 * (cp + 1), :], in_=wts[(h, cp)][:].rearrange("p u c i -> p (c i) u"))
 
         def w1_quantise(h):
             nc.vector.quantize_mx(out=w1c[:, h, :].bitcast(FP8X4), scales=w1s[:, h, :],
@@ -222,12 +217,12 @@ def tile_vfe_t_kernel(tc, voxel_feats, W0, gamma0, beta0, W1, gamma1, beta1, out
         zstp = {}
 
         def l0(k, t):
-            y0s[(k, t)] = ps_b([P, 512], F32, "y0") if (k < 3 and t < 2) else ps_a([P, 512], F32, "y0")
+            y0s[(k, t)] = ps_b([P, 512], F32, "y0") if (k < 4 and t < 2) else ps_a([P, 512], F32, "y0")
             nc.tensor.matmul(y0s[(k, t)][:], lhsT=w0t[:, t, :], rhs=xt[:, k, :], start=True, stop=True)
 
         def affine(k, t):
             if t == 0:
-                pts[k] = work.tile([P, 4, 512], BF16, name="pt")
+                pts[k] = work.tile([P, 4, 512], BF16, name="pt", bufs=5)
             if k == 0 and t % 2 == 1:
                 nc.vector.tensor_scalar(out=pts[k][:, t, :], in0=y0s[(k, t)][:], scalar1=s0[:, t:t + 1],
                                         scalar2=b0[:, t:t + 1], op0=ALU.mult, op1=ALU.add)
@@ -236,11 +231,10 @@ def tile_vfe_t_kernel(tc, voxel_feats, W0, gamma0, beta0, W1, gamma1, beta1, out
                                      bias=b0[:, t:t + 1], scale=s0[:, t:t + 1])
 
         def regroup(k):
-            grs[k] = work.tile([P, 512, 4], BF16, name="gr", align_bytes=64, bufs=1)
-            if k == 0:
-                nc.vector.tensor_scalar(out=grs[k][:].rearrange("p (c i) t -> p c t i", i=4),
-                                        in0=pts[k][:].rearrange("p t (c i) -> p c t i", i=4),
-                                        scalar1=0.0, scalar2=None, op0=ALU.max)
+            grs[k] = work.tile([P, 512, 4], BF16, name="gr", align_bytes=64, bufs=2)
+            if k < 2:
+                nc.vector.tensor_copy(out=grs[k][:].rearrange("p (c i) t -> p c t i", i=4),
+                                      in_=pts[k][:].rearrange("p t (c i) -> p c t i", i=4))
             else:
                 nc.gpsimd.tensor_scalar(out=grs[k][:], in0=pts[k][:].rearrange("p t r -> p r t"),
                                         scalar1=1.0, scalar2=0.0, op0=ALU.mult, op1=ALU.add)
@@ -256,11 +250,10 @@ def tile_vfe_t_kernel(tc, voxel_feats, W0, gamma0, beta0, W1, gamma1, beta1, out
 
         def amax(k):
             g, mb = divmod(k, BPG)
-            arf = arun[g][:].rearrange("p a r -> p (a r)")
             if mb == 0:
-                nc.vector.tensor_copy(out=arf, in_=flat_gr(k))
+                nc.vector.tensor_copy(out=arun[g][:], in_=pts[k][:])
             else:
-                nc.vector.tensor_tensor(out=arf, in0=arf, in1=flat_gr(k), op=ALU.max)
+                nc.vector.tensor_tensor(out=arun[g][:], in0=arun[g][:], in1=pts[k][:], op=ALU.max)
 
         def z_pass(k, ct):
             codes, scales = cds[k]
@@ -294,9 +287,11 @@ def tile_vfe_t_kernel(tc, voxel_feats, W0, gamma0, beta0, W1, gamma1, beta1, out
                                                in1=rmax[g][ct][:], op0=ALU.mult, op1=ALU.max)
 
         def group_a(g):
-            a1 = work.tile([P, 2, 512], BF16, name="a1")
-            nc.vector.tensor_tensor(out=a1[:], in0=arun[g][:, 0:2, :], in1=arun[g][:, 2:4, :], op=ALU.max)
-            nc.vector.tensor_tensor(out=agr[:, g, :], in0=a1[:, 0, :], in1=a1[:, 1, :], op=ALU.max)
+            a1 = work.tile([P, 4, 256], BF16, name="a1")
+            nc.vector.tensor_tensor(out=a1[:], in0=arun[g][:, :, 0:256], in1=arun[g][:, :, 256:512], op=ALU.max)
+            nc.vector.tensor_tensor(out=agr[:, g, :].rearrange("p (n t) -> p n t", t=4),
+                                    in0=a1[:, :, 0:128].rearrange("p t n -> p n t"),
+                                    in1=a1[:, :, 128:256].rearrange("p t n -> p n t"), op=ALU.max)
             nc.vector.quantize_mx(out=ac[:, g, :].bitcast(FP8X4), scales=asc[:, g, :], in_=agr[:, g, :])
 
         def group_zs_copy(g):
@@ -329,10 +324,12 @@ def tile_vfe_t_kernel(tc, voxel_feats, W0, gamma0, beta0, W1, gamma1, beta1, out
                                         lhsT_scale=w1s[:, 1, ct * P:(ct + 1) * P],
                                         rhs=acf.bitcast(FP8X4), rhs_scale=ascf, start=True, stop=True)
 
-        def quantise_and_max(k):
+        def quantise_block(k):
             quantise(k)
+
+        def running_max(k):
             amax(k)
-            if k == 3:
+            if k == NBLK - 2:
                 w1_quantise(1)
             if k % BPG == BPG - 1:
                 group_a(k // BPG)
@@ -340,6 +337,8 @@ def tile_vfe_t_kernel(tc, voxel_feats, W0, gamma0, beta0, W1, gamma1, beta1, out
         def sums_over_points(k):
             zsum_passes(k)
             if k == NBLK - 3:
+                w1_transposes(1, 0)
+                w1_transposes(1, 1)
                 group_zs_transposes(0)
             if k == NBLK - 1:
                 u_passes()
@@ -349,80 +348,98 @@ def tile_vfe_t_kernel(tc, voxel_feats, W0, gamma0, beta0, W1, gamma1, beta1, out
         for t in range(4):
             affine(0, t)
         w1_quantise(0)
+        nc.vector.tensor_scalar(out=pts[0][:, 1:4:2, :], in0=pts[0][:, 1:4:2, :], scalar1=0.0, scalar2=None, op0=ALU.max)
         regroup(0)
-        quantise_and_max(0)
+        quantise_block(0)
+        running_max(0)
+        xt_copy(3, "vector")
         for t in range(4):
             l0(1, t)
         for t in range(4):
             affine(1, t)
         regroup(1)
-        w1_transposes(1, 0)
-        w1_transposes(1, 1)
-        xt_copy(3, "vector")
-        w1_copy(1, 0)
-        w1_copy(1, 1)
+        quantise_block(1)
+        running_max(1)
         for t in range(4):
             l0(2, t)
+        l0(3, 0)
+        l0(3, 1)
         xt_transposes(4)
         xt_copy(4, "vector")
+        affine(2, 0)
+        affine(2, 1)
         z_pass(0, 0)
         z_pass(0, 1)
         sums_over_points(0)
-        for t in range(4):
-            affine(2, t)
-        l0(3, 0)
-        l0(3, 1)
+        affine(2, 2)
+        affine(2, 3)
+        regroup(2)
+        xt_transposes(5)
+        xt_copy(5, "vector")
+        affine(3, 0)
+        l0(3, 2)
+        affine(3, 1)
+        l0(3, 3)
+        affine(3, 2)
+        l0(4, 0)
+        affine(3, 3)
+        l0(4, 1)
 
         def have(k):
             return k < NBLK
 
         for i in range(NBLK):
-            if have(i + 2):
-                regroup(i + 2)
-            if have(i + 1):
-                quantise_and_max(i + 1)
+            if 1 <= i and have(i + 1):
+                quantise_block(i + 1)
             if have(i + 3):
-                affine(i + 3, 0)
+                regroup(i + 3)
+            if 1 <= i and have(i + 1):
+                running_max(i + 1)
+            if have(i + 4):
+                affine(i + 4, 0)
             square(i, 0)
             z_pass(i, 2)
-            if have(i + 3):
-                l0(i + 3, 2)
-                affine(i + 3, 1)
+            if have(i + 4):
+                l0(i + 4, 2)
+                affine(i + 4, 1)
             square(i, 1)
             z_pass(i, 3)
-            if have(i + 5):
-                xt_transposes(i + 5)
-            if have(i + 3):
-                l0(i + 3, 3)
+            if have(i + 6):
+                xt_transposes(i + 6)
+            if have(i + 4):
+                l0(i + 4, 3)
             if have(i + 1):
                 sums_over_points(i + 1)
             maxi(i, 0)
-            if have(i + 3):
-                affine(i + 3, 2)
-            square(i, 2)
             if have(i + 4):
-                l0(i + 4, 0)
+                affine(i + 4, 2)
+            square(i, 2)
+            if have(i + 5):
+                l0(i + 5, 0)
             if have(i + 1):
                 z_pass(i + 1, 0)
             maxi(i, 1)
-            if have(i + 3):
-                affine(i + 3, 3)
+            if have(i + 4):
+                affine(i + 4, 3)
             square(i, 3)
             if i == BPG - 2:
                 group_zs_copy(0)
+            if i == NBLK - 4:
+                w1_copy(1, 0)
+                w1_copy(1, 1)
             if i == NBLK - 3:
                 group_zs_sums(0)
             if i == NBLK - 2:
                 group_zs_copy(1)
                 group_zs_transposes(1)
                 group_zs_sums(1)
-            if have(i + 4):
-                l0(i + 4, 1)
+            if have(i + 5):
+                l0(i + 5, 1)
             if have(i + 1):
                 z_pass(i + 1, 1)
             maxi(i, 2)
-            if have(i + 5):
-                xt_copy(i + 5, "vector")
+            if have(i + 6):
+                xt_copy(i + 6, "vector")
             maxi(i, 3)
             if BPG <= i < BPG + 4:
                 group_rm(0, i - BPG)

@@ -347,43 +347,43 @@ def tile_vfe_t_kernel(tc, voxel_feats, W0, gamma0, beta0, W1, gamma1, beta1, out
             l0(0, t)
         for t in range(4):
             affine(0, t)
+        xt_copy(3, "vector")
         w1_quantise(0)
         nc.vector.tensor_scalar(out=pts[0][:, 1:4:2, :], in0=pts[0][:, 1:4:2, :], scalar1=0.0, scalar2=None, op0=ALU.max)
         regroup(0)
         quantise_block(0)
         running_max(0)
-        xt_copy(3, "vector")
         for t in range(4):
             l0(1, t)
         for t in range(4):
             affine(1, t)
-        regroup(1)
-        quantise_block(1)
-        running_max(1)
         for t in range(4):
             l0(2, t)
         l0(3, 0)
         l0(3, 1)
         xt_transposes(4)
         xt_copy(4, "vector")
+        regroup(1)
+        quantise_block(1)
+        running_max(1)
         affine(2, 0)
         affine(2, 1)
+        affine(2, 2)
+        l0(3, 2)
+        affine(2, 3)
+        l0(3, 3)
+        regroup(2)
         z_pass(0, 0)
         z_pass(0, 1)
-        sums_over_points(0)
-        affine(2, 2)
-        affine(2, 3)
-        regroup(2)
         xt_transposes(5)
         xt_copy(5, "vector")
         affine(3, 0)
-        l0(3, 2)
         affine(3, 1)
-        l0(3, 3)
         affine(3, 2)
         l0(4, 0)
         affine(3, 3)
         l0(4, 1)
+        sums_over_points(0)
 
         def have(k):
             return k < NBLK

@@ -17,6 +17,9 @@ NVOX = 256
 NPTS = 64
 ROWS = NVOX * NPTS
 EPS = 1e-3
+BIG = 3.4e38
+VC = 128
+GA0 = 20
 NBLK = 32
 BPG = 16
 
@@ -223,7 +226,12 @@ def tile_vfe_t_kernel(tc, voxel_feats, W0, gamma0, beta0, W1, gamma1, beta1, out
         def affine(k, t):
             if t == 0:
                 pts[k] = work.tile([P, 4, 512], BF16, name="pt", bufs=5)
-            if k == 0 and t % 2 == 1:
+            if k >= 4 and t == 3:
+                nc.scalar.activation(out=pts[k][:, t, 0:512 - VC], in_=y0s[(k, t)][:, 0:512 - VC], func=ACT.Relu,
+                                     bias=b0[:, t:t + 1], scale=s0[:, t:t + 1])
+                nc.vector.tensor_scalar(out=pts[k][:, t, 512 - VC:512], in0=y0s[(k, t)][:, 512 - VC:512], scalar1=s0[:, t:t + 1],
+                                        scalar2=b0[:, t:t + 1], op0=ALU.mult, op1=ALU.add)
+            elif k == 0 and t % 2 == 1:
                 nc.vector.tensor_scalar(out=pts[k][:, t, :], in0=y0s[(k, t)][:], scalar1=s0[:, t:t + 1],
                                         scalar2=b0[:, t:t + 1], op0=ALU.mult, op1=ALU.add)
             else:
@@ -237,7 +245,7 @@ def tile_vfe_t_kernel(tc, voxel_feats, W0, gamma0, beta0, W1, gamma1, beta1, out
                                       in_=pts[k][:].rearrange("p t (c i) -> p c t i", i=4))
             else:
                 nc.gpsimd.tensor_scalar(out=grs[k][:], in0=pts[k][:].rearrange("p t r -> p r t"),
-                                        scalar1=1.0, scalar2=0.0, op0=ALU.mult, op1=ALU.add)
+                                        scalar1=BIG, scalar2=0.0, op0=ALU.min, op1=ALU.max)
 
         def flat_gr(k):
             return grs[k][:].rearrange("p r t -> p (r t)")
@@ -251,7 +259,7 @@ def tile_vfe_t_kernel(tc, voxel_feats, W0, gamma0, beta0, W1, gamma1, beta1, out
         def amax(k):
             g, mb = divmod(k, BPG)
             if mb == 0:
-                nc.vector.tensor_copy(out=arun[g][:], in_=pts[k][:])
+                nc.vector.tensor_scalar(out=arun[g][:], in0=pts[k][:], scalar1=0.0, scalar2=None, op0=ALU.max)
             else:
                 nc.vector.tensor_tensor(out=arun[g][:], in0=arun[g][:], in1=pts[k][:], op=ALU.max)
 
@@ -286,13 +294,22 @@ def tile_vfe_t_kernel(tc, voxel_feats, W0, gamma0, beta0, W1, gamma1, beta1, out
                 nc.vector.scalar_tensor_tensor(out=rmax[g][ct][:], in0=z[:], scalar=sgn[:, ct:ct + 1],
                                                in1=rmax[g][ct][:], op0=ALU.mult, op1=ALU.max)
 
+        a1s = [keep.tile([P, 4, 256], BF16, name="a1_%d" % g) for g in range(2)]
+
+        def group_a_step(g, step):
+            a1 = a1s[g]
+            if step == 0:
+                nc.vector.tensor_tensor(out=a1[:], in0=arun[g][:, :, 0:256], in1=arun[g][:, :, 256:512], op=ALU.max)
+            elif step == 1:
+                nc.vector.tensor_tensor(out=agr[:, g, :].rearrange("p (n t) -> p n t", t=4),
+                                        in0=a1[:, :, 0:128].rearrange("p t n -> p n t"),
+                                        in1=a1[:, :, 128:256].rearrange("p t n -> p n t"), op=ALU.max)
+            else:
+                nc.vector.quantize_mx(out=ac[:, g, :].bitcast(FP8X4), scales=asc[:, g, :], in_=agr[:, g, :])
+
         def group_a(g):
-            a1 = work.tile([P, 4, 256], BF16, name="a1")
-            nc.vector.tensor_tensor(out=a1[:], in0=arun[g][:, :, 0:256], in1=arun[g][:, :, 256:512], op=ALU.max)
-            nc.vector.tensor_tensor(out=agr[:, g, :].rearrange("p (n t) -> p n t", t=4),
-                                    in0=a1[:, :, 0:128].rearrange("p t n -> p n t"),
-                                    in1=a1[:, :, 128:256].rearrange("p t n -> p n t"), op=ALU.max)
-            nc.vector.quantize_mx(out=ac[:, g, :].bitcast(FP8X4), scales=asc[:, g, :], in_=agr[:, g, :])
+            for step in range(3):
+                group_a_step(g, step)
 
         def group_zs_copy(g):
             nc.scalar.copy(out=zs_sb[g][:], in_=zsum[g][:])
@@ -331,8 +348,8 @@ def tile_vfe_t_kernel(tc, voxel_feats, W0, gamma0, beta0, W1, gamma1, beta1, out
             amax(k)
             if k == NBLK - 2:
                 w1_quantise(1)
-            if k % BPG == BPG - 1:
-                group_a(k // BPG)
+            if k == NBLK - 1:
+                group_a(1)
 
         def sums_over_points(k):
             zsum_passes(k)
@@ -443,6 +460,8 @@ def tile_vfe_t_kernel(tc, voxel_feats, W0, gamma0, beta0, W1, gamma1, beta1, out
             maxi(i, 3)
             if BPG <= i < BPG + 4:
                 group_rm(0, i - BPG)
+            if GA0 <= i < GA0 + 3:
+                group_a_step(0, i - GA0)
 
         for ct in range(4):
             u_ct = uts[ct // 2][:, ct % 2, :]

@@ -17,6 +17,8 @@ NVOX = 256
 NPTS = 64
 ROWS = NVOX * NPTS
 EPS = 1e-3
+VLO = 20
+VHI = 26
 BIG = 3.4e38
 VC = 128
 GA0 = 20
@@ -91,8 +93,8 @@ def tile_vfe_t_kernel(tc, voxel_feats, W0, gamma0, beta0, W1, gamma1, beta1, out
         be0 = keep.tile([P, 4], F32, name="be0")
         gb1 = keep.tile([P, 8], F32, name="gb1")
         pos = keep.tile([P, 4], F32, name="pos")
-        neg = keep.tile([P, 4], F32, name="neg")
         sgn = keep.tile([P, 4], F32, name="sgn")
+        gabs = keep.tile([P, 4], F32, name="gabs")
 
         def small_work(step):
             if step == 0:
@@ -106,9 +108,9 @@ def tile_vfe_t_kernel(tc, voxel_feats, W0, gamma0, beta0, W1, gamma1, beta1, out
                 nc.vector.tensor_copy(out=be0[:], in_=b0_bf[:])
                 nc.vector.tensor_copy(out=gb1[:], in_=gb1_ps[:, 0:8])
             elif step == 4:
-                nc.vector.tensor_scalar(out=pos[:], in0=gb1[:, 0:4], scalar1=0.0, scalar2=None, op0=ALU.is_gt)
-                nc.vector.tensor_scalar(out=neg[:], in0=gb1[:, 0:4], scalar1=0.0, scalar2=None, op0=ALU.is_lt)
-                nc.vector.tensor_tensor(out=sgn[:], in0=pos[:], in1=neg[:], op=ALU.subtract)
+                nc.vector.tensor_scalar(out=pos[:], in0=gb1[:, 0:4], scalar1=0.0, scalar2=None, op0=ALU.is_ge)
+                nc.vector.tensor_scalar(out=sgn[:], in0=pos[:], scalar1=2.0, scalar2=-1.0, op0=ALU.mult, op1=ALU.add)
+                nc.vector.tensor_tensor(out=gabs[:], in0=gb1[:, 0:4], in1=sgn[:], op=ALU.mult)
 
         g_ps = ps_c([P, 130], F32, "g_ps")
         for step, (g, m0, cnt) in enumerate(CHUNKS):
@@ -117,6 +119,9 @@ def tile_vfe_t_kernel(tc, voxel_feats, W0, gamma0, beta0, W1, gamma1, beta1, out
             for m in range(m0, m0 + cnt):
                 nc.tensor.matmul(g_ps[:], lhsT=x_sb[:, g, m, :], rhs=x_aug[:, g, m, :],
                                  start=(g == 0 and m == 0), stop=(g == 1 and m == NPTS - 1))
+
+        for ct in range(4):
+            nc.vector.tensor_scalar(out=w1_sb[:, ct, :], in0=w1_sb[:, ct, :], scalar1=sgn[:, ct:ct + 1], scalar2=None, op0=ALU.mult)
 
         xt = keep.tile([P, NBLK, 512], BF16, name="xt")
         xt_ps = ps_d([P, 2, 4, P], BF16, "xt_ps")
@@ -200,7 +205,7 @@ def tile_vfe_t_kernel(tc, voxel_feats, W0, gamma0, beta0, W1, gamma1, beta1, out
         w1_copy(0, 0)
         w1_copy(0, 1)
 
-        ssq = keep.tile([P, 4, NBLK], F32, name="ssq")
+        ssq = keep.tile([P, 4, NBLK + 3], F32, name="ssq")
         rmax = [[keep.tile([P, 512], F32, name="rmax%d%d" % (g, ct)) for ct in range(4)] for g in range(2)]
         rm = keep.tile([P, 4, 2, P], F32, name="rm")
         arun = [keep.tile([P, 4, 512], BF16, name="arun%d" % g) for g in range(2)]
@@ -209,8 +214,10 @@ def tile_vfe_t_kernel(tc, voxel_feats, W0, gamma0, beta0, W1, gamma1, beta1, out
         asc = keep.tile([P, 2, P], U8, name="asc", align_bytes=64)
         zs_sb = [keep.tile([P, 512], F32, name="zs_sb%d" % g) for g in range(2)]
         zst_sb = keep.tile([P, 4, 2, P], F32, name="zst_sb")
-        sacc = keep.tile([P, 4, 4], F32, name="sacc")
-        a3 = keep.tile([P, 4], F32, name="a3")
+        lsum = keep.tile([P, 4, 4], F32, name="lsum")
+        u_sb = keep.tile([P, 4, 2, P], F32, name="u_sb")
+        prod = keep.tile([P, 4, 2, P], F32, name="prod")
+        tmx = keep.tile([P, 4, 2, P], F32, name="tmx")
         y0s = {}
         pts = {}
         grs = {}
@@ -226,7 +233,7 @@ def tile_vfe_t_kernel(tc, voxel_feats, W0, gamma0, beta0, W1, gamma1, beta1, out
         def affine(k, t):
             if t == 0:
                 pts[k] = work.tile([P, 4, 512], BF16, name="pt", bufs=5)
-            if k >= 4 and t == 3:
+            if k >= 4 and t == 3 and not (VLO <= k <= VHI):
                 nc.scalar.activation(out=pts[k][:, t, 0:512 - VC], in_=y0s[(k, t)][:, 0:512 - VC], func=ACT.Relu,
                                      bias=b0[:, t:t + 1], scale=s0[:, t:t + 1])
                 nc.vector.tensor_scalar(out=pts[k][:, t, 512 - VC:512], in0=y0s[(k, t)][:, 512 - VC:512], scalar1=s0[:, t:t + 1],
@@ -289,10 +296,9 @@ def tile_vfe_t_kernel(tc, voxel_feats, W0, gamma0, beta0, W1, gamma1, beta1, out
             g, mb = divmod(k, BPG)
             z = zts[(k, ct)]
             if mb == 0:
-                nc.vector.tensor_scalar(out=rmax[g][ct][:], in0=z[:], scalar1=sgn[:, ct:ct + 1], scalar2=None, op0=ALU.mult)
+                nc.vector.tensor_copy(out=rmax[g][ct][:], in_=z[:])
             else:
-                nc.vector.scalar_tensor_tensor(out=rmax[g][ct][:], in0=z[:], scalar=sgn[:, ct:ct + 1],
-                                               in1=rmax[g][ct][:], op0=ALU.mult, op1=ALU.max)
+                nc.vector.tensor_tensor(out=rmax[g][ct][:], in0=z[:], in1=rmax[g][ct][:], op=ALU.max)
 
         a1s = [keep.tile([P, 4, 256], BF16, name="a1_%d" % g) for g in range(2)]
 
@@ -321,44 +327,34 @@ def tile_vfe_t_kernel(tc, voxel_feats, W0, gamma0, beta0, W1, gamma1, beta1, out
 
         def group_zs_sums(g):
             for ct in range(4):
-                nc.scalar.activation(out=zst_sb[:, ct, g, :], in_=zstp[g][:, ct, :], func=ACT.Copy, accum_out=sacc[:, g, ct:ct + 1])
+                nc.scalar.activation(out=zst_sb[:, ct, g, :], in_=zstp[g][:, ct, :], func=ACT.Copy, scale=1.0 / NPTS, accum_out=lsum[:, g, ct:ct + 1])
+
+        def group_u_copies(g):
+            for ct in range(4):
+                nc.scalar.activation(out=u_sb[:, ct, g, :], in_=uts[g][:, ct, :], func=ACT.Copy, accum_out=lsum[:, 2 + g, ct:ct + 1])
+
+        def group_u_squares(g):
+            for ct in range(4):
+                junk_b = work.tile([P, P], BF16, name="junk_b")
+                nc.scalar.activation(out=junk_b[:], in_=uts[g][:, ct, :], func=ACT.Square, scale=8.0, accum_out=ssq[:, ct, NBLK + g:NBLK + g + 1])
+
+        def cross_sums():
+            for ct in range(4):
+                junk_c = work.tile([P, 256], BF16, name="junk_c")
+                nc.scalar.activation(out=junk_c[:], in_=prod[:, ct, :, :].rearrange("p g n -> p (g n)"), func=ACT.Copy, scale=2.0 * NPTS, accum_out=ssq[:, ct, NBLK + 2:NBLK + 3])
 
         def group_rm(g, ct):
             nc.vector.tensor_reduce(out=rm[:, ct, g, :], in_=rmax[g][ct][:].rearrange("p (a n) -> p n a", a=4),
                                     axis=AX.X, op=ALU.max)
 
-        uts = []
+        uts = {}
 
-        def u_passes():
-            acf = ac[:].rearrange("p g n -> p (g n)")
-            ascf = asc[:].rearrange("p g n -> p (g n)")
-            for cp in range(2):
-                ut = ps_a([P, 2, 256], F32, "ut")
-                uts.append(ut)
-                for cc in range(2):
-                    ct = 2 * cp + cc
-                    nc.tensor.matmul_mx(out=ut[:, cc, :], lhsT=w1c[:, 1, ct * P:(ct + 1) * P].bitcast(FP8X4),
-                                        lhsT_scale=w1s[:, 1, ct * P:(ct + 1) * P],
-                                        rhs=acf.bitcast(FP8X4), rhs_scale=ascf, start=True, stop=True)
-
-        def quantise_block(k):
-            quantise(k)
-
-        def running_max(k):
-            amax(k)
-            if k == NBLK - 2:
-                w1_quantise(1)
-            if k == NBLK - 1:
-                group_a(1)
-
-        def sums_over_points(k):
-            zsum_passes(k)
-            if k == NBLK - 3:
-                w1_transposes(1, 0)
-                w1_transposes(1, 1)
-                group_zs_transposes(0)
-            if k == NBLK - 1:
-                u_passes()
+        def u_passes(g):
+            uts[g] = ps_a([P, 4, P], F32, "ut")
+            for ct in range(4):
+                nc.tensor.matmul_mx(out=uts[g][:, ct, :], lhsT=w1c[:, 1, ct * P:(ct + 1) * P].bitcast(FP8X4),
+                                    lhsT_scale=w1s[:, 1, ct * P:(ct + 1) * P],
+                                    rhs=ac[:, g, :].bitcast(FP8X4), rhs_scale=asc[:, g, :], start=True, stop=True)
 
         for t in range(4):
             l0(0, t)
@@ -368,8 +364,8 @@ def tile_vfe_t_kernel(tc, voxel_feats, W0, gamma0, beta0, W1, gamma1, beta1, out
         w1_quantise(0)
         nc.vector.tensor_scalar(out=pts[0][:, 1:4:2, :], in0=pts[0][:, 1:4:2, :], scalar1=0.0, scalar2=None, op0=ALU.max)
         regroup(0)
-        quantise_block(0)
-        running_max(0)
+        quantise(0)
+        amax(0)
         for t in range(4):
             l0(1, t)
         for t in range(4):
@@ -381,8 +377,8 @@ def tile_vfe_t_kernel(tc, voxel_feats, W0, gamma0, beta0, W1, gamma1, beta1, out
         xt_transposes(4)
         xt_copy(4, "vector")
         regroup(1)
-        quantise_block(1)
-        running_max(1)
+        quantise(1)
+        amax(1)
         affine(2, 0)
         affine(2, 1)
         affine(2, 2)
@@ -400,60 +396,42 @@ def tile_vfe_t_kernel(tc, voxel_feats, W0, gamma0, beta0, W1, gamma1, beta1, out
         l0(4, 0)
         affine(3, 3)
         l0(4, 1)
-        sums_over_points(0)
+        zsum_passes(0)
 
         def have(k):
             return k < NBLK
 
-        for i in range(NBLK):
-            if 1 <= i and have(i + 1):
-                quantise_block(i + 1)
-            if have(i + 3):
-                regroup(i + 3)
-            if 1 <= i and have(i + 1):
-                running_max(i + 1)
-            if have(i + 4):
-                affine(i + 4, 0)
+        for i in range(NBLK - 4):
+            if i >= 1:
+                quantise(i + 1)
+            regroup(i + 3)
+            if i >= 1:
+                amax(i + 1)
+            affine(i + 4, 0)
             square(i, 0)
             z_pass(i, 2)
-            if have(i + 4):
-                l0(i + 4, 2)
-                affine(i + 4, 1)
+            l0(i + 4, 2)
+            affine(i + 4, 1)
             square(i, 1)
             z_pass(i, 3)
             if have(i + 6):
                 xt_transposes(i + 6)
-            if have(i + 4):
-                l0(i + 4, 3)
-            if have(i + 1):
-                sums_over_points(i + 1)
+            l0(i + 4, 3)
+            zsum_passes(i + 1)
             maxi(i, 0)
-            if have(i + 4):
-                affine(i + 4, 2)
+            affine(i + 4, 2)
             square(i, 2)
             if have(i + 5):
                 l0(i + 5, 0)
-            if have(i + 1):
-                z_pass(i + 1, 0)
+            z_pass(i + 1, 0)
             maxi(i, 1)
-            if have(i + 4):
-                affine(i + 4, 3)
+            affine(i + 4, 3)
             square(i, 3)
             if i == BPG - 2:
                 group_zs_copy(0)
-            if i == NBLK - 4:
-                w1_copy(1, 0)
-                w1_copy(1, 1)
-            if i == NBLK - 3:
-                group_zs_sums(0)
-            if i == NBLK - 2:
-                group_zs_copy(1)
-                group_zs_transposes(1)
-                group_zs_sums(1)
             if have(i + 5):
                 l0(i + 5, 1)
-            if have(i + 1):
-                z_pass(i + 1, 1)
+            z_pass(i + 1, 1)
             maxi(i, 2)
             if have(i + 6):
                 xt_copy(i + 6, "vector")
@@ -463,42 +441,120 @@ def tile_vfe_t_kernel(tc, voxel_feats, W0, gamma0, beta0, W1, gamma1, beta1, out
             if GA0 <= i < GA0 + 3:
                 group_a_step(0, i - GA0)
 
+        i = NBLK - 4
+        quantise(i + 1)
+        regroup(i + 3)
+        amax(i + 1)
+        square(i, 0)
+        z_pass(i, 2)
+        square(i, 1)
+        z_pass(i, 3)
+        zsum_passes(i + 1)
+        w1_transposes(1, 0)
+        w1_transposes(1, 1)
+        group_zs_transposes(0)
+        maxi(i, 0)
+        square(i, 2)
+        z_pass(i + 1, 0)
+        maxi(i, 1)
+        square(i, 3)
+        w1_copy(1, 0)
+        w1_copy(1, 1)
+        group_zs_sums(0)
+        z_pass(i + 1, 1)
+        maxi(i, 2)
+        maxi(i, 3)
+
+        i = NBLK - 3
+        quantise(i + 1)
+        amax(i + 1)
+        w1_quantise(1)
+        square(i, 0)
+        z_pass(i, 2)
+        square(i, 1)
+        z_pass(i, 3)
+        zsum_passes(i + 1)
+        u_passes(0)
+        maxi(i, 0)
+        square(i, 2)
+        z_pass(i + 1, 0)
+        maxi(i, 1)
+        square(i, 3)
+        group_u_copies(0)
+        group_u_squares(0)
+        z_pass(i + 1, 1)
+        maxi(i, 2)
+        maxi(i, 3)
+
+        i = NBLK - 2
+        quantise(i + 1)
+        amax(i + 1)
+        group_a(1)
+        square(i, 0)
+        z_pass(i, 2)
+        square(i, 1)
+        z_pass(i, 3)
+        zsum_passes(i + 1)
+        square(i, 2)
+        square(i, 3)
+        group_zs_copy(1)
+        group_zs_transposes(1)
+        group_zs_sums(1)
+        u_passes(1)
+        group_u_copies(1)
+        nc.gpsimd.tensor_tensor(out=prod[:], in0=u_sb[:], in1=zst_sb[:], op=ALU.mult)
+        nc.gpsimd.tensor_tensor(out=tmx[:, :, 0, :], in0=rm[:, :, 0, :], in1=u_sb[:, :, 0, :], op=ALU.add)
+        maxi(i, 0)
+        z_pass(i + 1, 0)
+        maxi(i, 1)
+        z_pass(i + 1, 1)
+        maxi(i, 2)
+        z_pass(i + 1, 2)
+        maxi(i, 3)
+        z_pass(i + 1, 3)
+
+        def small(name):
+            return keep.tile([P, 4], F32, name=name)
+
+        i = NBLK - 1
         for ct in range(4):
-            u_ct = uts[ct // 2][:, ct % 2, :]
-            junk_a = work.tile([P, 256], BF16, name="junk_a")
-            nc.scalar.activation(out=junk_a[:], in_=u_ct, func=ACT.Copy, accum_out=sacc[:, 2, ct:ct + 1])
-            junk_b = work.tile([P, 256], BF16, name="junk_b")
-            nc.scalar.activation(out=junk_b[:], in_=u_ct, func=ACT.Square, accum_out=sacc[:, 3, ct:ct + 1])
-        for ct in range(4):
-            group_rm(1, ct)
-        for ct in range(4):
-            junk_c = work.tile([P, 256], F32, name="junk_c")
-            nc.vector.scalar_tensor_tensor(out=junk_c[:], in0=uts[ct // 2][:, ct % 2, :], scalar=1.0,
-                                           in1=zst_sb[:, ct, :, :].rearrange("p g n -> p (g n)"),
-                                           op0=ALU.mult, op1=ALU.mult, accum_out=a3[:, ct:ct + 1])
-        ssqt = keep.tile([P, 4], F32, name="ssqt")
-        nc.vector.tensor_reduce(out=ssqt[:], in_=ssq[:], axis=AX.X, op=ALU.add)
-        lin0 = keep.tile([P, 4], F32, name="lin0")
-        nc.vector.tensor_tensor(out=lin0[:], in0=sacc[:, 0, :], in1=sacc[:, 1, :], op=ALU.add)
-        lin = keep.tile([P, 4], F32, name="lin")
-        nc.vector.scalar_tensor_tensor(out=lin[:], in0=sacc[:, 2, :], scalar=float(NPTS), in1=lin0[:], op0=ALU.mult, op1=ALU.add)
-        mean1 = keep.tile([P, 4], F32, name="mean1")
-        nc.vector.tensor_scalar(out=mean1[:], in0=lin[:], scalar1=1.0 / ROWS, scalar2=None, op0=ALU.mult)
-        half = keep.tile([P, 4], F32, name="half")
-        nc.vector.scalar_tensor_tensor(out=half[:], in0=sacc[:, 3, :], scalar=0.5 * NPTS, in1=a3[:], op0=ALU.mult, op1=ALU.add)
-        q1 = keep.tile([P, 4], F32, name="q1")
-        nc.vector.scalar_tensor_tensor(out=q1[:], in0=half[:], scalar=2.0, in1=ssqt[:], op0=ALU.mult, op1=ALU.add)
-        s1, b1 = scale_and_shift(q1[:], mean1[:], gb1[:, 0:4], gb1[:, 4:8], "1")
-        s1abs = keep.tile([P, 4], F32, name="s1abs")
-        nc.vector.tensor_tensor(out=s1abs[:], in0=s1[:], in1=sgn[:], op=ALU.mult)
+            square(i, ct)
+            maxi(i, ct)
+        group_u_squares(1)
+        cross_sums()
+        group_rm(1, 0)
+        linp = small("linp")
+        nc.vector.tensor_reduce(out=linp[:], in_=lsum[:].rearrange("p r c -> p c r"), axis=AX.X, op=ALU.add)
+        group_rm(1, 1)
+        msq1 = small("msq1")
+        nc.vector.scalar_tensor_tensor(out=msq1[:], in0=linp[:], scalar=(float(NPTS) / ROWS) * (float(NPTS) / ROWS), in1=linp[:], op0=ALU.mult, op1=ALU.mult)
+        negm = small("negm")
+        nc.vector.scalar_tensor_tensor(out=negm[:], in0=linp[:], scalar=-float(NPTS) / ROWS, in1=gabs[:], op0=ALU.mult, op1=ALU.mult)
+        q1 = small("q1")
+        nc.vector.tensor_reduce(out=q1[:], in_=ssq[:], axis=AX.X, op=ALU.add)
+        group_rm(1, 2)
+        var1 = small("var1")
+        nc.vector.scalar_tensor_tensor(out=var1[:], in0=q1[:], scalar=1.0 / ROWS, in1=msq1[:], op0=ALU.mult, op1=ALU.subtract)
+        group_rm(1, 3)
+        nc.vector.tensor_scalar(out=var1[:], in0=var1[:], scalar1=0.0, scalar2=EPS, op0=ALU.max, op1=ALU.add)
+        std1 = small("std1")
+        nc.scalar.activation(out=std1[:], in_=var1[:], func=ACT.Sqrt)
+        nc.vector.tensor_tensor(out=tmx[:, :, 1, :], in0=rm[:, :, 1, :], in1=u_sb[:, :, 1, :], op=ALU.add)
+        rstd1 = small("rstd1")
+        nc.vector.reciprocal(out=rstd1[:], in_=std1[:])
+        s1 = small("s1")
+        nc.vector.tensor_tensor(out=s1[:], in0=gabs[:], in1=rstd1[:], op=ALU.mult)
+        b1 = small("b1")
+        nc.vector.tensor_tensor(out=b1[:], in0=negm[:], in1=rstd1[:], op=ALU.mult)
+        nc.vector.tensor_tensor(out=b1[:], in0=b1[:], in1=gb1[:, 4:8], op=ALU.add)
 
         fin = keep.tile([P, 4, 2, P], F32, name="fin")
         for ct in range(4):
-            wsb = work.tile([P, 256], F32, name="wsb")
-            nc.scalar.activation(out=wsb[:], in_=uts[ct // 2][:, ct % 2, :], func=ACT.Identity, bias=b1[:, ct:ct + 1], scale=s1[:, ct:ct + 1])
-            nc.vector.scalar_tensor_tensor(out=fin[:, ct, :, :].rearrange("p g n -> p (g n)"),
-                                           in0=rm[:, ct, :, :].rearrange("p g n -> p (g n)"),
-                                           scalar=s1abs[:, ct:ct + 1], in1=wsb[:], op0=ALU.mult, op1=ALU.add)
+            if ct < 2:
+                nc.scalar.activation(out=fin[:, ct, :, :], in_=tmx[:, ct, :, :], func=ACT.Identity, bias=b1[:, ct:ct + 1], scale=s1[:, ct:ct + 1])
+            else:
+                nc.vector.tensor_scalar(out=fin[:, ct, :, :], in0=tmx[:, ct, :, :], scalar1=s1[:, ct:ct + 1], scalar2=b1[:, ct:ct + 1],
+                                        op0=ALU.mult, op1=ALU.add)
         for g in range(2):
             o_ps = ps_b([P, 512], F32, "o_ps")
             for ct in range(4):

@@ -251,7 +251,8 @@ def tile_vfe_t_kernel(tc, voxel_feats, W0, gamma0, beta0, W1, gamma1, beta1, out
                 nc.vector.tensor_copy(out=grs[k][:].rearrange("p (c i) t -> p c t i", i=4),
                                       in_=pts[k][:].rearrange("p t (c i) -> p c t i", i=4))
             else:
-                nc.gpsimd.tensor_scalar(out=grs[k][:], in0=pts[k][:].rearrange("p t r -> p r t"),
+                nc.gpsimd.tensor_scalar(out=grs[k][:].rearrange("p (c i) t -> p c t i", i=4),
+                                        in0=pts[k][:].rearrange("p t (c i) -> p c t i", i=4),
                                         scalar1=BIG, scalar2=0.0, op0=ALU.min, op1=ALU.max)
 
         def flat_gr(k):

@@ -20,7 +20,7 @@ EPS = 1e-3
 VLO = 20
 VHI = 26
 BIG = 3.4e38
-VC = 128
+VC = 224
 GA0 = 20
 NBLK = 32
 BPG = 16

@@ -120,8 +120,10 @@ def tile_vfe_t_kernel(tc, voxel_feats, W0, gamma0, beta0, W1, gamma1, beta1, out
                 nc.tensor.matmul(g_ps[:], lhsT=x_sb[:, g, m, :], rhs=x_aug[:, g, m, :],
                                  start=(g == 0 and m == 0), stop=(g == 1 and m == NPTS - 1))
 
-        for ct in range(4):
-            nc.vector.tensor_scalar(out=w1_sb[:, ct, :], in0=w1_sb[:, ct, :], scalar1=sgn[:, ct:ct + 1], scalar2=None, op0=ALU.mult)
+        def w1_signs(h):
+            for ct in range(4):
+                half = w1_sb[:, ct, 512 * h:512 * (h + 1)]
+                nc.vector.tensor_scalar(out=half, in0=half, scalar1=sgn[:, ct:ct + 1], scalar2=None, op0=ALU.mult)
 
         xt = keep.tile([P, NBLK, 512], BF16, name="xt")
         xt_ps = ps_d([P, 2, 4, P], BF16, "xt_ps")
@@ -158,27 +160,10 @@ def tile_vfe_t_kernel(tc, voxel_feats, W0, gamma0, beta0, W1, gamma1, beta1, out
             nc.vector.quantize_mx(out=w1c[:, h, :].bitcast(FP8X4), scales=w1s[:, h, :],
                                   in_=w1g[:, h, :, :].rearrange("p c t -> p (c t)"))
 
-        def scale_and_shift(sumsq, mean, gam, bet, label):
-            msq = keep.tile([P, 4], F32, name="msq" + label)
-            nc.vector.tensor_tensor(out=msq[:], in0=mean, in1=mean, op=ALU.mult)
-            var = keep.tile([P, 4], F32, name="var" + label)
-            nc.vector.scalar_tensor_tensor(out=var[:], in0=sumsq, scalar=1.0 / ROWS, in1=msq[:], op0=ALU.mult, op1=ALU.subtract)
-            nc.vector.tensor_scalar(out=var[:], in0=var[:], scalar1=0.0, scalar2=EPS, op0=ALU.max, op1=ALU.add)
-            std = keep.tile([P, 4], F32, name="std" + label)
-            nc.scalar.activation(out=std[:], in_=var[:], func=ACT.Sqrt)
-            rstd = keep.tile([P, 4], F32, name="rstd" + label)
-            nc.vector.reciprocal(out=rstd[:], in_=std[:])
-            scl = keep.tile([P, 4], F32, name="scl" + label)
-            nc.vector.tensor_tensor(out=scl[:], in0=gam, in1=rstd[:], op=ALU.mult)
-            msc = keep.tile([P, 4], F32, name="msc" + label)
-            nc.vector.tensor_tensor(out=msc[:], in0=mean, in1=scl[:], op=ALU.mult)
-            sft = keep.tile([P, 4], F32, name="sft" + label)
-            nc.vector.tensor_tensor(out=sft[:], in0=bet, in1=msc[:], op=ALU.subtract)
-            return scl, sft
-
         xt_transposes(0)
         gs = keep.tile([P, 130], F32, name="gs")
         nc.vector.tensor_copy(out=gs[:], in_=g_ps[:])
+        w1_signs(0)
         tqs = []
         for h in range(2):
             tq = ps_a([P, 2, 130], F32, "tq")
@@ -195,13 +180,37 @@ def tile_vfe_t_kernel(tc, voxel_feats, W0, gamma0, beta0, W1, gamma1, beta1, out
         xt_transposes(3)
         q0 = keep.tile([P, 4], F32, name="q0")
         mean0 = keep.tile([P, 4], F32, name="mean0")
-        for t in range(4):
+        msq0 = keep.tile([P, 4], F32, name="msq0")
+        gm0 = keep.tile([P, 4], F32, name="gm0")
+        var0 = keep.tile([P, 4], F32, name="var0")
+        rstd0 = keep.tile([P, 4], F32, name="rstd0")
+        s0 = keep.tile([P, 4], F32, name="s0")
+        b0 = keep.tile([P, 4], F32, name="b0")
+
+        def q0_product(t):
             junk_q = work.tile([P, P], F32, name="junk_q")
             nc.vector.scalar_tensor_tensor(out=junk_q[:], in0=tqs[t // 2][:, t % 2, 0:128], scalar=1.0, in1=w0_f[:, t, :],
                                            op0=ALU.mult, op1=ALU.mult, accum_out=q0[:, t:t + 1])
-        for h in range(2):
+
+        def mean0_half(h):
             nc.vector.tensor_scalar(out=mean0[:, 2 * h:2 * h + 2], in0=tqs[h][:, :, 128], scalar1=1.0 / ROWS, scalar2=None, op0=ALU.mult)
-        s0, b0 = scale_and_shift(q0[:], mean0[:], g0[:], be0[:], "0")
+
+        q0_product(0)
+        mean0_half(0)
+        q0_product(1)
+        mean0_half(1)
+        q0_product(2)
+        nc.vector.tensor_tensor(out=msq0[:], in0=mean0[:], in1=mean0[:], op=ALU.mult)
+        nc.vector.scalar_tensor_tensor(out=gm0[:], in0=mean0[:], scalar=-1.0, in1=g0[:], op0=ALU.mult, op1=ALU.mult)
+        q0_product(3)
+        nc.vector.scalar_tensor_tensor(out=var0[:], in0=q0[:], scalar=1.0 / ROWS, in1=msq0[:], op0=ALU.mult, op1=ALU.subtract)
+        nc.vector.tensor_scalar(out=var0[:], in0=var0[:], scalar1=0.0, scalar2=EPS, op0=ALU.max, op1=ALU.add)
+        std0 = keep.tile([P, 4], F32, name="std0")
+        nc.scalar.activation(out=std0[:], in_=var0[:], func=ACT.Sqrt)
+        nc.vector.reciprocal(out=rstd0[:], in_=std0[:])
+        nc.vector.tensor_tensor(out=b0[:], in0=gm0[:], in1=rstd0[:], op=ALU.mult)
+        nc.vector.tensor_tensor(out=s0[:], in0=g0[:], in1=rstd0[:], op=ALU.mult)
+        nc.vector.tensor_tensor(out=b0[:], in0=b0[:], in1=be0[:], op=ALU.add)
         w1_copy(0, 0)
         w1_copy(0, 1)
 
@@ -362,11 +371,12 @@ def tile_vfe_t_kernel(tc, voxel_feats, W0, gamma0, beta0, W1, gamma1, beta1, out
         for t in range(4):
             affine(0, t)
         xt_copy(3, "vector")
+        w1_signs(1)
         w1_quantise(0)
         nc.vector.tensor_scalar(out=pts[0][:, 1:4:2, :], in0=pts[0][:, 1:4:2, :], scalar1=0.0, scalar2=None, op0=ALU.max)
         regroup(0)
-        quantise(0)
         amax(0)
+        quantise(0)
         for t in range(4):
             l0(1, t)
         for t in range(4):
@@ -378,8 +388,8 @@ def tile_vfe_t_kernel(tc, voxel_feats, W0, gamma0, beta0, W1, gamma1, beta1, out
         xt_transposes(4)
         xt_copy(4, "vector")
         regroup(1)
-        quantise(1)
         amax(1)
+        quantise(1)
         affine(2, 0)
         affine(2, 1)
         affine(2, 2)
@@ -565,4 +575,7 @@ def tile_vfe_t_kernel(tc, voxel_feats, W0, gamma0, beta0, W1, gamma1, beta1, out
                 nc.scalar.activation(out=o_sb[:], in_=o_ps[:], func=ACT.Relu)
             else:
                 nc.vector.tensor_scalar(out=o_sb[:], in0=o_ps[:], scalar1=0.0, scalar2=None, op0=ALU.max)
-            nc.sync.dma_start(out=out[g * P:(g + 1) * P, :], in_=o_sb[:])
+            if g == 0:
+                nc.sync.dma_start(out=out[g * P:(g + 1) * P, :], in_=o_sb[:])
+            else:
+                nc.scalar.dma_start(out=out[g * P:(g + 1) * P, :], in_=o_sb[:])

@@ -25,7 +25,7 @@ GA0 = 20
 NBLK = 32
 BPG = 16
 
-CHUNKS = [(0, 0, 8), (0, 8, 8), (0, 16, 16), (0, 32, 16), (0, 48, 16), (1, 0, 16), (1, 16, 16), (1, 32, 16), (1, 48, 8), (1, 56, 8)]
+CHUNKS = [(g, m, 8) for g in range(2) for m in range(0, 64, 8)]
 
 FLOPS = 2 * (ROWS * 128 * 512 + ROWS * 512 * 512 + NVOX * 512 * 512)
 
@@ -82,10 +82,7 @@ def tile_vfe_t_kernel(tc, voxel_feats, W0, gamma0, beta0, W1, gamma1, beta1, out
         nc.vector.memset(x_aug[:, :, :, 128:130], 1.0)
 
         w0t_ps = ps_a([P, 4, P], BF16, "w0t_ps")
-        for t in range(4):
-            nc.tensor.transpose(w0t_ps[:, t, :], w0_sb[:, t, :], ident_bf[:])
         gb1_ps = ps_a([P, P], BF16, "gb1_ps")
-        nc.tensor.transpose(gb1_ps[:], gb1_rows[:], ident_bf[:])
         w0t = keep.tile([P, 4, P], BF16, name="w0t")
         w0t_f = keep.tile([P, 4, P], F32, name="w0t_f")
         w0_f = keep.tile([P, 4, P], F32, name="w0_f")
@@ -97,28 +94,33 @@ def tile_vfe_t_kernel(tc, voxel_feats, W0, gamma0, beta0, W1, gamma1, beta1, out
         gabs = keep.tile([P, 4], F32, name="gabs")
 
         def small_work(step):
-            if step == 0:
-                nc.vector.tensor_copy(out=w0t[:], in_=w0t_ps[:])
-            elif step == 1:
-                nc.vector.tensor_copy(out=w0t_f[:], in_=w0t_ps[:])
-            elif step == 2:
+            if step == 4:
+                for t in range(4):
+                    nc.tensor.transpose(w0t_ps[:, t, :], w0_sb[:, t, :], ident_bf[:])
+                nc.tensor.transpose(gb1_ps[:], gb1_rows[:], ident_bf[:])
                 nc.vector.tensor_copy(out=w0_f[:], in_=w0_sb[:])
-            elif step == 3:
+            elif step == 6:
+                nc.vector.tensor_copy(out=w0t[:], in_=w0t_ps[:])
+            elif step == 7:
+                nc.vector.tensor_copy(out=w0t_f[:], in_=w0t_ps[:])
+            elif step == 8:
                 nc.vector.tensor_copy(out=g0[:], in_=g0_bf[:])
                 nc.vector.tensor_copy(out=be0[:], in_=b0_bf[:])
                 nc.vector.tensor_copy(out=gb1[:], in_=gb1_ps[:, 0:8])
-            elif step == 4:
+            elif step == 10:
                 nc.vector.tensor_scalar(out=pos[:], in0=gb1[:, 0:4], scalar1=0.0, scalar2=None, op0=ALU.is_ge)
+            elif step == 11:
                 nc.vector.tensor_scalar(out=sgn[:], in0=pos[:], scalar1=2.0, scalar2=-1.0, op0=ALU.mult, op1=ALU.add)
+            elif step == 12:
                 nc.vector.tensor_tensor(out=gabs[:], in0=gb1[:, 0:4], in1=sgn[:], op=ALU.mult)
 
         g_ps = ps_c([P, 130], F32, "g_ps")
         for step, (g, m0, cnt) in enumerate(CHUNKS):
             nc.vector.tensor_copy(out=x_aug[:, g, m0:m0 + cnt, 0:128], in_=x_sb[:, g, m0:m0 + cnt, :])
-            small_work(step)
             for m in range(m0, m0 + cnt):
                 nc.tensor.matmul(g_ps[:], lhsT=x_sb[:, g, m, :], rhs=x_aug[:, g, m, :],
                                  start=(g == 0 and m == 0), stop=(g == 1 and m == NPTS - 1))
+            small_work(step)
 
         def w1_signs(h):
             for ct in range(4):

@@ -122,9 +122,9 @@ def tile_vfe_t_kernel(tc, voxel_feats, W0, gamma0, beta0, W1, gamma1, beta1, out
                                  start=(g == 0 and m == 0), stop=(g == 1 and m == NPTS - 1))
             small_work(step)
 
-        def w1_signs(h):
+        def w1_signs():
             for ct in range(4):
-                half = w1_sb[:, ct, 512 * h:512 * (h + 1)]
+                half = w1_sb[:, ct, 0:512]
                 nc.vector.tensor_scalar(out=half, in0=half, scalar1=sgn[:, ct:ct + 1], scalar2=None, op0=ALU.mult)
 
         xt = keep.tile([P, NBLK, 512], BF16, name="xt")
@@ -165,7 +165,7 @@ def tile_vfe_t_kernel(tc, voxel_feats, W0, gamma0, beta0, W1, gamma1, beta1, out
         xt_transposes(0)
         gs = keep.tile([P, 130], F32, name="gs")
         nc.vector.tensor_copy(out=gs[:], in_=g_ps[:])
-        w1_signs(0)
+        w1_signs()
         tqs = []
         for h in range(2):
             tq = ps_a([P, 2, 130], F32, "tq")
@@ -217,7 +217,8 @@ def tile_vfe_t_kernel(tc, voxel_feats, W0, gamma0, beta0, W1, gamma1, beta1, out
         w1_copy(0, 1)
 
         ssq = keep.tile([P, 4, NBLK + 3], F32, name="ssq")
-        rmax = [[keep.tile([P, 512], F32, name="rmax%d%d" % (g, ct)) for ct in range(4)] for g in range(2)]
+        rmax = [keep.tile([P, 4, 512], F32, name="rmax%d" % g) for g in range(2)]
+        rh = keep.tile([P, 4, 256], F32, name="rh")
         rm = keep.tile([P, 4, 2, P], F32, name="rm")
         arun = [keep.tile([P, 4, 512], BF16, name="arun%d" % g) for g in range(2)]
         agr = keep.tile([P, 2, 512], BF16, name="agr", align_bytes=64)
@@ -259,8 +260,9 @@ def tile_vfe_t_kernel(tc, voxel_feats, W0, gamma0, beta0, W1, gamma1, beta1, out
         def regroup(k):
             grs[k] = work.tile([P, 512, 4], BF16, name="gr", align_bytes=64, bufs=2)
             if k < 2:
-                nc.vector.tensor_copy(out=grs[k][:].rearrange("p (c i) t -> p c t i", i=4),
-                                      in_=pts[k][:].rearrange("p t (c i) -> p c t i", i=4))
+                nc.vector.tensor_scalar(out=grs[k][:].rearrange("p (c i) t -> p c t i", i=4),
+                                        in0=pts[k][:].rearrange("p t (c i) -> p c t i", i=4),
+                                        scalar1=0.0, scalar2=None, op0=ALU.max)
             else:
                 nc.gpsimd.tensor_scalar(out=grs[k][:].rearrange("p (c i) t -> p c t i", i=4),
                                         in0=pts[k][:].rearrange("p t (c i) -> p c t i", i=4),
@@ -308,9 +310,9 @@ def tile_vfe_t_kernel(tc, voxel_feats, W0, gamma0, beta0, W1, gamma1, beta1, out
             g, mb = divmod(k, BPG)
             z = zts[(k, ct)]
             if mb == 0:
-                nc.vector.tensor_copy(out=rmax[g][ct][:], in_=z[:])
+                nc.vector.tensor_copy(out=rmax[g][:, ct, :], in_=z[:])
             else:
-                nc.vector.tensor_tensor(out=rmax[g][ct][:], in0=z[:], in1=rmax[g][ct][:], op=ALU.max)
+                nc.vector.tensor_tensor(out=rmax[g][:, ct, :], in0=z[:], in1=rmax[g][:, ct, :], op=ALU.max)
 
         a1s = [keep.tile([P, 4, 256], BF16, name="a1_%d" % g) for g in range(2)]
 
@@ -343,7 +345,7 @@ def tile_vfe_t_kernel(tc, voxel_feats, W0, gamma0, beta0, W1, gamma1, beta1, out
 
         def group_u_copies(g):
             for ct in range(4):
-                nc.scalar.activation(out=u_sb[:, ct, g, :], in_=uts[g][:, ct, :], func=ACT.Copy, accum_out=lsum[:, 2 + g, ct:ct + 1])
+                nc.scalar.activation(out=u_sb[:, ct, g, :], in_=uts[g][:, ct, :], func=ACT.Copy, scale=sgn[:, ct:ct + 1], accum_out=lsum[:, 2 + g, ct:ct + 1])
 
         def group_u_squares(g):
             for ct in range(4):
@@ -355,9 +357,11 @@ def tile_vfe_t_kernel(tc, voxel_feats, W0, gamma0, beta0, W1, gamma1, beta1, out
                 junk_c = work.tile([P, 256], BF16, name="junk_c")
                 nc.scalar.activation(out=junk_c[:], in_=prod[:, ct, :, :].rearrange("p g n -> p (g n)"), func=ACT.Copy, scale=2.0 * NPTS, accum_out=ssq[:, ct, NBLK + 2:NBLK + 3])
 
-        def group_rm(g, ct):
-            nc.vector.tensor_reduce(out=rm[:, ct, g, :], in_=rmax[g][ct][:].rearrange("p (a n) -> p n a", a=4),
-                                    axis=AX.X, op=ALU.max)
+        def group_rm(g, step):
+            if step == 0:
+                nc.vector.tensor_tensor(out=rh[:], in0=rmax[g][:, :, 0:256], in1=rmax[g][:, :, 256:512], op=ALU.max)
+            else:
+                nc.vector.tensor_tensor(out=rm[:, :, g, :], in0=rh[:, :, 0:128], in1=rh[:, :, 128:256], op=ALU.max)
 
         uts = {}
 
@@ -373,9 +377,7 @@ def tile_vfe_t_kernel(tc, voxel_feats, W0, gamma0, beta0, W1, gamma1, beta1, out
         for t in range(4):
             affine(0, t)
         xt_copy(3, "vector")
-        w1_signs(1)
         w1_quantise(0)
-        nc.vector.tensor_scalar(out=pts[0][:, 1:4:2, :], in0=pts[0][:, 1:4:2, :], scalar1=0.0, scalar2=None, op0=ALU.max)
         regroup(0)
         amax(0)
         quantise(0)
@@ -449,7 +451,7 @@ def tile_vfe_t_kernel(tc, voxel_feats, W0, gamma0, beta0, W1, gamma1, beta1, out
             if have(i + 6):
                 xt_copy(i + 6, "vector")
             maxi(i, 3)
-            if BPG <= i < BPG + 4:
+            if BPG <= i < BPG + 2:
                 group_rm(0, i - BPG)
             if GA0 <= i < GA0 + 3:
                 group_a_step(0, i - GA0)
@@ -538,17 +540,15 @@ def tile_vfe_t_kernel(tc, voxel_feats, W0, gamma0, beta0, W1, gamma1, beta1, out
         group_rm(1, 0)
         linp = small("linp")
         nc.vector.tensor_reduce(out=linp[:], in_=lsum[:].rearrange("p r c -> p c r"), axis=AX.X, op=ALU.add)
-        group_rm(1, 1)
         msq1 = small("msq1")
         nc.vector.scalar_tensor_tensor(out=msq1[:], in0=linp[:], scalar=(float(NPTS) / ROWS) * (float(NPTS) / ROWS), in1=linp[:], op0=ALU.mult, op1=ALU.mult)
         negm = small("negm")
         nc.vector.scalar_tensor_tensor(out=negm[:], in0=linp[:], scalar=-float(NPTS) / ROWS, in1=gabs[:], op0=ALU.mult, op1=ALU.mult)
         q1 = small("q1")
         nc.vector.tensor_reduce(out=q1[:], in_=ssq[:], axis=AX.X, op=ALU.add)
-        group_rm(1, 2)
         var1 = small("var1")
         nc.vector.scalar_tensor_tensor(out=var1[:], in0=q1[:], scalar=1.0 / ROWS, in1=msq1[:], op0=ALU.mult, op1=ALU.subtract)
-        group_rm(1, 3)
+        group_rm(1, 1)
         nc.vector.tensor_scalar(out=var1[:], in0=var1[:], scalar1=0.0, scalar2=EPS, op0=ALU.max, op1=ALU.add)
         std1 = small("std1")
         nc.scalar.activation(out=std1[:], in_=var1[:], func=ACT.Sqrt)
@@ -563,21 +563,21 @@ def tile_vfe_t_kernel(tc, voxel_feats, W0, gamma0, beta0, W1, gamma1, beta1, out
 
         fin = keep.tile([P, 4, 2, P], F32, name="fin")
         for ct in range(4):
-            if ct < 2:
+            if ct < 1:
                 nc.scalar.activation(out=fin[:, ct, :, :], in_=tmx[:, ct, :, :], func=ACT.Identity, bias=b1[:, ct:ct + 1], scale=s1[:, ct:ct + 1])
             else:
                 nc.vector.tensor_scalar(out=fin[:, ct, :, :], in0=tmx[:, ct, :, :], scalar1=s1[:, ct:ct + 1], scalar2=b1[:, ct:ct + 1],
                                         op0=ALU.mult, op1=ALU.add)
         for g in range(2):
             o_ps = ps_b([P, 512], F32, "o_ps")
-            for ct in range(4):
+            for ct in (1, 2, 3, 0):
                 nc.tensor.transpose(o_ps[:, ct * P:(ct + 1) * P], fin[:, ct, g, :], ident_f[:])
-            o_sb = work.tile([P, 512], F32, name="o_sb")
-            if g == 0:
-                nc.scalar.activation(out=o_sb[:], in_=o_ps[:], func=ACT.Relu)
-            else:
-                nc.vector.tensor_scalar(out=o_sb[:], in0=o_ps[:], scalar1=0.0, scalar2=None, op0=ALU.max)
-            if g == 0:
-                nc.sync.dma_start(out=out[g * P:(g + 1) * P, :], in_=o_sb[:])
-            else:
-                nc.scalar.dma_start(out=out[g * P:(g + 1) * P, :], in_=o_sb[:])
+            for half in (1, 0):
+                cols = slice(256 * half, 256 * half + 256)
+                o_sb = work.tile([P, 256], F32, name="o_sb%d" % half, bufs=2)
+                if g == 0:
+                    nc.scalar.activation(out=o_sb[:], in_=o_ps[:, cols], func=ACT.Relu)
+                    nc.sync.dma_start(out=out[g * P:(g + 1) * P, cols], in_=o_sb[:])
+                else:
+                    nc.vector.tensor_scalar(out=o_sb[:], in0=o_ps[:, cols], scalar1=0.0, scalar2=None, op0=ALU.max)
+                    nc.scalar.dma_start(out=out[g * P:(g + 1) * P, cols], in_=o_sb[:])

@@ -17,6 +17,7 @@ NVOX = 256
 NPTS = 64
 ROWS = NVOX * NPTS
 EPS = 1e-3
+RMAX = EPS ** -0.5
 VLO = 20
 VHI = 26
 BIG = 3.4e38
@@ -73,7 +74,7 @@ def tile_vfe_t_kernel(tc, voxel_feats, W0, gamma0, beta0, W1, gamma1, beta1, out
         one_col = keep.tile([P, 1], F32, name="one_col")
         nc.vector.memset(one_col[:], 1.0)
         warm = keep.tile([P, 1], F32, name="warm")
-        nc.scalar.activation(out=warm[:], in_=one_col[:], func=ACT.Sqrt)
+        nc.scalar.activation(out=warm[:], in_=one_col[:], func=ACT.Abs_reciprocal_sqrt)
         ident_bf = keep.tile([P, P], BF16, name="ident_bf")
         make_identity(nc, ident_bf[:])
         ident_f = keep.tile([P, P], F32, name="ident_f")
@@ -207,9 +208,7 @@ def tile_vfe_t_kernel(tc, voxel_feats, W0, gamma0, beta0, W1, gamma1, beta1, out
         q0_product(3)
         nc.vector.scalar_tensor_tensor(out=var0[:], in0=q0[:], scalar=1.0 / ROWS, in1=msq0[:], op0=ALU.mult, op1=ALU.subtract)
         nc.vector.tensor_scalar(out=var0[:], in0=var0[:], scalar1=0.0, scalar2=EPS, op0=ALU.max, op1=ALU.add)
-        std0 = keep.tile([P, 4], F32, name="std0")
-        nc.scalar.activation(out=std0[:], in_=var0[:], func=ACT.Sqrt)
-        nc.vector.reciprocal(out=rstd0[:], in_=std0[:])
+        nc.scalar.activation(out=rstd0[:], in_=var0[:], func=ACT.Abs_reciprocal_sqrt)
         nc.vector.tensor_tensor(out=b0[:], in0=gm0[:], in1=rstd0[:], op=ALU.mult)
         nc.vector.tensor_tensor(out=s0[:], in0=g0[:], in1=rstd0[:], op=ALU.mult)
         nc.vector.tensor_tensor(out=b0[:], in0=b0[:], in1=be0[:], op=ALU.add)
@@ -464,10 +463,10 @@ def tile_vfe_t_kernel(tc, voxel_feats, W0, gamma0, beta0, W1, gamma1, beta1, out
         z_pass(i, 2)
         square(i, 1)
         z_pass(i, 3)
-        zsum_passes(i + 1)
         w1_transposes(1, 0)
         w1_transposes(1, 1)
         group_zs_transposes(0)
+        zsum_passes(i + 1)
         maxi(i, 0)
         square(i, 2)
         z_pass(i + 1, 0)
@@ -481,21 +480,22 @@ def tile_vfe_t_kernel(tc, voxel_feats, W0, gamma0, beta0, W1, gamma1, beta1, out
         maxi(i, 3)
 
         i = NBLK - 3
+        w1_quantise(1)
         quantise(i + 1)
         amax(i + 1)
-        w1_quantise(1)
         square(i, 0)
         z_pass(i, 2)
         square(i, 1)
         z_pass(i, 3)
-        zsum_passes(i + 1)
         u_passes(0)
+        zsum_passes(i + 1)
         maxi(i, 0)
         square(i, 2)
         z_pass(i + 1, 0)
         maxi(i, 1)
         square(i, 3)
         group_u_copies(0)
+        nc.gpsimd.tensor_tensor(out=tmx[:, :, 0, :], in0=rm[:, :, 0, :], in1=u_sb[:, :, 0, :], op=ALU.add)
         group_u_squares(0)
         z_pass(i + 1, 1)
         maxi(i, 2)
@@ -518,7 +518,6 @@ def tile_vfe_t_kernel(tc, voxel_feats, W0, gamma0, beta0, W1, gamma1, beta1, out
         u_passes(1)
         group_u_copies(1)
         nc.gpsimd.tensor_tensor(out=prod[:], in0=u_sb[:], in1=zst_sb[:], op=ALU.mult)
-        nc.gpsimd.tensor_tensor(out=tmx[:, :, 0, :], in0=rm[:, :, 0, :], in1=u_sb[:, :, 0, :], op=ALU.add)
         maxi(i, 0)
         z_pass(i + 1, 0)
         maxi(i, 1)
@@ -537,28 +536,26 @@ def tile_vfe_t_kernel(tc, voxel_feats, W0, gamma0, beta0, W1, gamma1, beta1, out
             maxi(i, ct)
         group_u_squares(1)
         cross_sums()
-        group_rm(1, 0)
         linp = small("linp")
-        nc.vector.tensor_reduce(out=linp[:], in_=lsum[:].rearrange("p r c -> p c r"), axis=AX.X, op=ALU.add)
         msq1 = small("msq1")
-        nc.vector.scalar_tensor_tensor(out=msq1[:], in0=linp[:], scalar=(float(NPTS) / ROWS) * (float(NPTS) / ROWS), in1=linp[:], op0=ALU.mult, op1=ALU.mult)
         negm = small("negm")
-        nc.vector.scalar_tensor_tensor(out=negm[:], in0=linp[:], scalar=-float(NPTS) / ROWS, in1=gabs[:], op0=ALU.mult, op1=ALU.mult)
         q1 = small("q1")
-        nc.vector.tensor_reduce(out=q1[:], in_=ssq[:], axis=AX.X, op=ALU.add)
         var1 = small("var1")
-        nc.vector.scalar_tensor_tensor(out=var1[:], in0=q1[:], scalar=1.0 / ROWS, in1=msq1[:], op0=ALU.mult, op1=ALU.subtract)
-        group_rm(1, 1)
-        nc.vector.tensor_scalar(out=var1[:], in0=var1[:], scalar1=0.0, scalar2=EPS, op0=ALU.max, op1=ALU.add)
-        std1 = small("std1")
-        nc.scalar.activation(out=std1[:], in_=var1[:], func=ACT.Sqrt)
-        nc.vector.tensor_tensor(out=tmx[:, :, 1, :], in0=rm[:, :, 1, :], in1=u_sb[:, :, 1, :], op=ALU.add)
         rstd1 = small("rstd1")
-        nc.vector.reciprocal(out=rstd1[:], in_=std1[:])
         s1 = small("s1")
-        nc.vector.tensor_tensor(out=s1[:], in0=gabs[:], in1=rstd1[:], op=ALU.mult)
         b1 = small("b1")
-        nc.vector.tensor_tensor(out=b1[:], in0=negm[:], in1=rstd1[:], op=ALU.mult)
+        nc.vector.tensor_reduce(out=linp[:], in_=lsum[:].rearrange("p r c -> p c r"), axis=AX.X, op=ALU.add)
+        group_rm(1, 0)
+        nc.vector.scalar_tensor_tensor(out=msq1[:], in0=linp[:], scalar=(float(NPTS) / ROWS) * (float(NPTS) / ROWS), in1=linp[:], op0=ALU.mult, op1=ALU.mult)
+        nc.vector.scalar_tensor_tensor(out=negm[:], in0=linp[:], scalar=-float(NPTS) / ROWS, in1=gabs[:], op0=ALU.mult, op1=ALU.mult)
+        group_rm(1, 1)
+        nc.vector.tensor_scalar(out=msq1[:], in0=msq1[:], scalar1=EPS, scalar2=None, op0=ALU.subtract)
+        nc.vector.tensor_reduce(out=q1[:], in_=ssq[:], axis=AX.X, op=ALU.add)
+        nc.vector.scalar_tensor_tensor(out=var1[:], in0=q1[:], scalar=1.0 / ROWS, in1=msq1[:], op0=ALU.mult, op1=ALU.subtract)
+        nc.scalar.activation(out=rstd1[:], in_=var1[:], func=ACT.Abs_reciprocal_sqrt)
+        nc.vector.tensor_tensor(out=tmx[:, :, 1, :], in0=rm[:, :, 1, :], in1=u_sb[:, :, 1, :], op=ALU.add)
+        nc.vector.scalar_tensor_tensor(out=b1[:], in0=rstd1[:], scalar=RMAX, in1=negm[:], op0=ALU.min, op1=ALU.mult)
+        nc.vector.scalar_tensor_tensor(out=s1[:], in0=rstd1[:], scalar=RMAX, in1=gabs[:], op0=ALU.min, op1=ALU.mult)
         nc.vector.tensor_tensor(out=b1[:], in0=b1[:], in1=gb1[:, 4:8], op=ALU.add)
 
         fin = keep.tile([P, 4, 2, P], F32, name="fin")

from contextlib import ExitStack

import concourse.mybir as mybir
from concourse.masks import make_identity

FP8X4 = mybir.dt.float8_e4m3fn_x4
BF16 = mybir.dt.bfloat16
F32 = mybir.dt.float32
U32 = mybir.dt.uint32
U8 = mybir.dt.uint8
ACT = mybir.ActivationFunctionType
ALU = mybir.AluOpType
AX = mybir.AxisListType

P = 128
NVOX = 256
NPTS = 64
ROWS = NVOX * NPTS
EPS = 1e-3
RMAX = EPS ** -0.5
VLO = 20
VHI = 26
BIG = 3.4e38
VC = 224
GA0 = 20
NBLK = 32
BPG = 16

CHUNKS = [(g, m, 8) for g in range(2) for m in range(0, 64, 8)]

FLOPS = 2 * (ROWS * 128 * 512 + ROWS * 512 * 512 + NVOX * 512 * 512)


def tile_vfe_t_kernel(tc, voxel_feats, W0, gamma0, beta0, W1, gamma1, beta1, out):
    nc = tc.nc
    with ExitStack() as ctx:
        ctx.enter_context(tc.manual_schedule())
        keep = ctx.enter_context(tc.tile_pool(name="keep", bufs=1))
        work = ctx.enter_context(tc.tile_pool(name="work", bufs=3))
        psum = ctx.enter_context(tc.psum_pool(name="psum", bufs=1))

        def ps_a(shape, dtype, name):
            return psum.tile(shape, dtype, name=name, tag="a", bufs=2)

        def ps_b(shape, dtype, name):
            return psum.tile(shape, dtype, name=name, tag="b", bufs=4)

        def ps_c(shape, dtype, name):
            return psum.tile(shape, dtype, name=name, tag="c", bufs=1)

        def ps_d(shape, dtype, name):
            return psum.tile(shape, dtype, name=name, tag="d", bufs=1)

        x_sb = keep.tile([P, 2, NPTS, 128], BF16, name="x_sb")
        xv = voxel_feats.rearrange("(g n) m c -> n g m c", g=2)
        for g, m0, cnt in CHUNKS:
            nc.sync.dma_start(out=x_sb[:, g, m0:m0 + cnt, :], in_=xv[:, g, m0:m0 + cnt, :])
        w1_sb = keep.tile([P, 4, 1024], BF16, name="w1_sb")
        w1v = W1.rearrange("(ct i) k -> i ct k", ct=4)
        for hh in range(2):
            nc.sync.dma_start(out=w1_sb[:, 2 * hh:2 * hh + 2, :], in_=w1v[:, 2 * hh:2 * hh + 2, :])

        w0_sb = keep.tile([P, 4, 128], BF16, name="w0_sb")
        nc.scalar.dma_start(out=w0_sb[:], in_=W0.rearrange("(j t) c -> j t c", t=4))
        g0_bf = keep.tile([P, 4], BF16, name="g0_bf")
        nc.scalar.dma_start(out=g0_bf[:], in_=gamma0.rearrange("(j t) -> j t", t=4))
        b0_bf = keep.tile([P, 4], BF16, name="b0_bf")
        nc.scalar.dma_start(out=b0_bf[:], in_=beta0.rearrange("(j t) -> j t", t=4))
        gb1_rows = keep.tile([P, P], BF16, name="gb1_rows")
        nc.vector.memset(gb1_rows[:], 0.0)
        nc.scalar.dma_start(out=gb1_rows[0:4, :], in_=gamma1.rearrange("(r i) -> r i", r=4))
        nc.scalar.dma_start(out=gb1_rows[4:8, :], in_=beta1.rearrange("(r i) -> r i", r=4))

        one_col = keep.tile([P, 1], F32, name="one_col")
        nc.vector.memset(one_col[:], 1.0)
        warm = keep.tile([P, 1], F32, name="warm")
        nc.scalar.activation(out=warm[:], in_=one_col[:], func=ACT.Abs_reciprocal_sqrt)
        ident_bf = keep.tile([P, P], BF16, name="ident_bf")
        make_identity(nc, ident_bf[:])
        ident_f = keep.tile([P, P], F32, name="ident_f")
        make_identity(nc, ident_f[:])
        x_aug = keep.tile([P, 2, NPTS, 130], BF16, name="x_aug")
        nc.vector.memset(x_aug[:, :, :, 128:130], 1.0)

        w0t_ps = ps_a([P, 4, P], BF16, "w0t_ps")
        gb1_ps = ps_a([P, P], BF16, "gb1_ps")
        w0t = keep.tile([P, 4, P], BF16, name="w0t")
        w0t_f = keep.tile([P, 4, P], F32, name="w0t_f")
        w0_f = keep.tile([P, 4, P], F32, name="w0_f")
        g0 = keep.tile([P, 4], F32, name="g0")
        be0 = keep.tile([P, 4], F32, name="be0")
        gb1 = keep.tile([P, 8], F32, name="gb1")
        pos = keep.tile([P, 4], F32, name="pos")
        sgn = keep.tile([P, 4], F32, name="sgn")
        gabs = keep.tile([P, 4], F32, name="gabs")

        def small_work(step):
            if step == 4:
                for t in range(4):
                    nc.tensor.transpose(w0t_ps[:, t, :], w0_sb[:, t, :], ident_bf[:])
                nc.tensor.transpose(gb1_ps[:], gb1_rows[:], ident_bf[:])
                nc.vector.tensor_copy(out=w0_f[:], in_=w0_sb[:])
            elif step == 6:
                nc.vector.tensor_copy(out=w0t[:], in_=w0t_ps[:])
            elif step == 7:
                nc.vector.tensor_copy(out=w0t_f[:], in_=w0t_ps[:])
            elif step == 8:
                nc.vector.tensor_copy(out=g0[:], in_=g0_bf[:])
                nc.vector.tensor_copy(out=be0[:], in_=b0_bf[:])
                nc.vector.tensor_copy(out=gb1[:], in_=gb1_ps[:, 0:8])
            elif step == 10:
                nc.vector.tensor_scalar(out=pos[:], in0=gb1[:, 0:4], scalar1=0.0, scalar2=None, op0=ALU.is_ge)
            elif step == 11:
                nc.vector.tensor_scalar(out=sgn[:], in0=pos[:], scalar1=2.0, scalar2=-1.0, op0=ALU.mult, op1=ALU.add)
            elif step == 12:
                nc.vector.tensor_tensor(out=gabs[:], in0=gb1[:, 0:4], in1=sgn[:], op=ALU.mult)

        g_ps = ps_c([P, 130], F32, "g_ps")
        for step, (g, m0, cnt) in enumerate(CHUNKS):
            nc.vector.tensor_copy(out=x_aug[:, g, m0:m0 + cnt, 0:128], in_=x_sb[:, g, m0:m0 + cnt, :])
            for m in range(m0, m0 + cnt):
                nc.tensor.matmul(g_ps[:], lhsT=x_sb[:, g, m, :], rhs=x_aug[:, g, m, :],
                                 start=(g == 0 and m == 0), stop=(g == 1 and m == NPTS - 1))
            small_work(step)

        def w1_signs():
            for ct in range(4):
                half = w1_sb[:, ct, 0:512]
                nc.vector.tensor_scalar(out=half, in0=half, scalar1=sgn[:, ct:ct + 1], scalar2=None, op0=ALU.mult)

        xt = keep.tile([P, NBLK, 512], BF16, name="xt")
        xt_ps = ps_d([P, 2, 4, P], BF16, "xt_ps")

        def xt_transposes(k):
            g, mb = divmod(k, BPG)
            for mi in range(4):
                nc.tensor.transpose(xt_ps[:, k % 2, mi, :], x_sb[:, g, 4 * mb + mi, :], ident_bf[:])

        def xt_copy(k, engine):
            flat = xt_ps[:, k % 2, :, :].rearrange("p a r -> p (a r)")
            if engine == "scalar":
                nc.scalar.copy(out=xt[:, k, :], in_=flat)
            else:
                nc.vector.tensor_copy(out=xt[:, k, :], in_=flat)

        w1w = w1_sb[:].bitcast(F32)
        w1g = keep.tile([P, 2, 512, 4], BF16, name="w1g", align_bytes=64)
        w1gw = w1g[:].bitcast(F32)
        w1c = keep.tile([P, 2, 512], U32, name="w1c", align_bytes=64)
        w1s = keep.tile([P, 2, 512], U8, name="w1s", align_bytes=64)
        wts = {}

        def w1_transposes(h, cp):
            wts[(h, cp)] = ps_b([P, 2, 2, P], F32, "wt_ps") if h == 0 else ps_a([P, 2, 2, P], F32, "wt_ps")
            for u in range(2):
                for cc in range(2):
                    nc.tensor.transpose(wts[(h, cp)][:, u, cc, :], w1w[:, 2 * cp + cc, 256 * h + u:256 * h + 256:2], ident_f[:])

        def w1_copy(h, cp):
            nc.scalar.copy(out=w1gw[:, h, 256 * cp:256 * (cp + 1), :], in_=wts[(h, cp)][:].rearrange("p u c i -> p (c i) u"))

        def w1_quantise(h):
            nc.vector.quantize_mx(out=w1c[:, h, :].bitcast(FP8X4), scales=w1s[:, h, :],
                                  in_=w1g[:, h, :, :].rearrange("p c t -> p (c t)"))

        xt_transposes(0)
        gs = keep.tile([P, 130], F32, name="gs")
        nc.vector.tensor_copy(out=gs[:], in_=g_ps[:])
        w1_signs()
        tqs = []
        for h in range(2):
            tq = ps_a([P, 2, 130], F32, "tq")
            tqs.append(tq)
            for tt in range(2):
                nc.tensor.matmul(tq[:, tt, :], lhsT=w0t_f[:, 2 * h + tt, :], rhs=gs[:], start=True, stop=True)
        xt_copy(0, "scalar")
        xt_transposes(1)
        xt_copy(1, "scalar")
        xt_transposes(2)
        xt_copy(2, "scalar")
        w1_transposes(0, 0)
        w1_transposes(0, 1)
        xt_transposes(3)
        q0 = keep.tile([P, 4], F32, name="q0")
        mean0 = keep.tile([P, 4], F32, name="mean0")
        msq0 = keep.tile([P, 4], F32, name="msq0")
        gm0 = keep.tile([P, 4], F32, name="gm0")
        var0 = keep.tile([P, 4], F32, name="var0")
        rstd0 = keep.tile([P, 4], F32, name="rstd0")
        s0 = keep.tile([P, 4], F32, name="s0")
        b0 = keep.tile([P, 4], F32, name="b0")

        def q0_product(t):
            junk_q = work.tile([P, P], F32, name="junk_q")
            nc.vector.scalar_tensor_tensor(out=junk_q[:], in0=tqs[t // 2][:, t % 2, 0:128], scalar=1.0, in1=w0_f[:, t, :],
                                           op0=ALU.mult, op1=ALU.mult, accum_out=q0[:, t:t + 1])

        def mean0_half(h):
            nc.vector.tensor_scalar(out=mean0[:, 2 * h:2 * h + 2], in0=tqs[h][:, :, 128], scalar1=1.0 / ROWS, scalar2=None, op0=ALU.mult)

        q0_product(0)
        mean0_half(0)
        q0_product(1)
        mean0_half(1)
        q0_product(2)
        nc.vector.tensor_tensor(out=msq0[:], in0=mean0[:], in1=mean0[:], op=ALU.mult)
        nc.vector.scalar_tensor_tensor(out=gm0[:], in0=mean0[:], scalar=-1.0, in1=g0[:], op0=ALU.mult, op1=ALU.mult)
        q0_product(3)
        nc.vector.scalar_tensor_tensor(out=var0[:], in0=q0[:], scalar=1.0 / ROWS, in1=msq0[:], op0=ALU.mult, op1=ALU.subtract)
        nc.vector.tensor_scalar(out=var0[:], in0=var0[:], scalar1=0.0, scalar2=EPS, op0=ALU.max, op1=ALU.add)
        nc.scalar.activation(out=rstd0[:], in_=var0[:], func=ACT.Abs_reciprocal_sqrt)
        nc.vector.tensor_tensor(out=b0[:], in0=gm0[:], in1=rstd0[:], op=ALU.mult)
        nc.vector.tensor_tensor(out=s0[:], in0=g0[:], in1=rstd0[:], op=ALU.mult)
        nc.vector.tensor_tensor(out=b0[:], in0=b0[:], in1=be0[:], op=ALU.add)
        w1_copy(0, 0)
        w1_copy(0, 1)

        ssq = keep.tile([P, 4, NBLK + 3], F32, name="ssq")
        rmax = [keep.tile([P, 4, 512], F32, name="rmax%d" % g) for g in range(2)]
        rh = keep.tile([P, 4, 256], F32, name="rh")
        rm = keep.tile([P, 4, 2, P], F32, name="rm")
        arun = [keep.tile([P, 4, 512], BF16, name="arun%d" % g) for g in range(2)]
        agr = keep.tile([P, 2, 512], BF16, name="agr", align_bytes=64)
        ac = keep.tile([P, 2, P], U32, name="ac", align_bytes=64)
        asc = keep.tile([P, 2, P], U8, name="asc", align_bytes=64)
        zs_sb = [keep.tile([P, 512], F32, name="zs_sb%d" % g) for g in range(2)]
        zst_sb = keep.tile([P, 4, 2, P], F32, name="zst_sb")
        lsum = keep.tile([P, 4, 4], F32, name="lsum")
        u_sb = keep.tile([P, 4, 2, P], F32, name="u_sb")
        prod = keep.tile([P, 4, 2, P], F32, name="prod")
        tmx = keep.tile([P, 4, 2, P], F32, name="tmx")
        y0s = {}
        pts = {}
        grs = {}
        cds = {}
        zts = {}
        zsum = {}
        zstp = {}

        def l0(k, t):
            y0s[(k, t)] = ps_b([P, 512], F32, "y0") if (k < 4 and t < 2) else ps_a([P, 512], F32, "y0")
            nc.tensor.matmul(y0s[(k, t)][:], lhsT=w0t[:, t, :], rhs=xt[:, k, :], start=True, stop=True)

        def affine(k, t):
            if t == 0:
                pts[k] = work.tile([P, 4, 512], BF16, name="pt", bufs=5)
            if k >= 4 and t == 3 and not (VLO <= k <= VHI):
                nc.scalar.activation(out=pts[k][:, t, 0:512 - VC], in_=y0s[(k, t)][:, 0:512 - VC], func=ACT.Relu,
                                     bias=b0[:, t:t + 1], scale=s0[:, t:t + 1])
                nc.vector.tensor_scalar(out=pts[k][:, t, 512 - VC:512], in0=y0s[(k, t)][:, 512 - VC:512], scalar1=s0[:, t:t + 1],
                                        scalar2=b0[:, t:t + 1], op0=ALU.mult, op1=ALU.add)
            elif k == 0 and t % 2 == 1:
                nc.vector.tensor_scalar(out=pts[k][:, t, :], in0=y0s[(k, t)][:], scalar1=s0[:, t:t + 1],
                                        scalar2=b0[:, t:t + 1], op0=ALU.mult, op1=ALU.add)
            else:
                nc.scalar.activation(out=pts[k][:, t, :], in_=y0s[(k, t)][:], func=ACT.Relu,
                                     bias=b0[:, t:t + 1], scale=s0[:, t:t + 1])

        def regroup(k):
            grs[k] = work.tile([P, 512, 4], BF16, name="gr", align_bytes=64, bufs=2)
            if k < 2:
                nc.vector.tensor_scalar(out=grs[k][:].rearrange("p (c i) t -> p c t i", i=4),
                                        in0=pts[k][:].rearrange("p t (c i) -> p c t i", i=4),
                                        scalar1=0.0, scalar2=None, op0=ALU.max)
            else:
                nc.gpsimd.tensor_scalar(out=grs[k][:].rearrange("p (c i) t -> p c t i", i=4),
                                        in0=pts[k][:].rearrange("p t (c i) -> p c t i", i=4),
                                        scalar1=BIG, scalar2=0.0, op0=ALU.min, op1=ALU.max)

        def flat_gr(k):
            return grs[k][:].rearrange("p r t -> p (r t)")

        def quantise(k):
            codes = work.tile([P, 512], U32, name="codes", align_bytes=64)
            scales = work.tile([P, 512], U8, name="scales", align_bytes=64)
            cds[k] = (codes, scales)
            nc.vector.quantize_mx(out=codes[:].bitcast(FP8X4), scales=scales[:], in_=flat_gr(k))

        def amax(k):
            g, mb = divmod(k, BPG)
            if mb == 0:
                nc.vector.tensor_scalar(out=arun[g][:], in0=pts[k][:], scalar1=0.0, scalar2=None, op0=ALU.max)
            else:
                nc.vector.tensor_tensor(out=arun[g][:], in0=arun[g][:], in1=pts[k][:], op=ALU.max)

        def z_pass(k, ct):
            codes, scales = cds[k]
            zts[(k, ct)] = ps_b([P, 512], F32, "z")
            nc.tensor.matmul_mx(out=zts[(k, ct)][:], lhsT=w1c[:, 0, ct * P:(ct + 1) * P].bitcast(FP8X4),
                                lhsT_scale=w1s[:, 0, ct * P:(ct + 1) * P],
                                rhs=codes[:].bitcast(FP8X4), rhs_scale=scales[:], start=True, stop=True)

        def zsum_passes(k):
            g, mb = divmod(k, BPG)
            codes, scales = cds[k]
            if mb == 0:
                zsum[g] = ps_c([P, 512], F32, "zs_ps")
            for mi in range(4):
                nc.tensor.matmul_mx(out=zsum[g][:], lhsT=codes[:, mi * P:(mi + 1) * P].bitcast(FP8X4),
                                    lhsT_scale=scales[:, mi * P:(mi + 1) * P],
                                    rhs=w1c[:, 0, :].bitcast(FP8X4), rhs_scale=w1s[:, 0, :],
                                    start=(mb == 0 and mi == 0), stop=(mb == BPG - 1 and mi == 3))

        def square(k, ct):
            junk = work.tile([P, 512], BF16, name="junk")
            nc.scalar.activation(out=junk[:], in_=zts[(k, ct)][:], func=ACT.Square, accum_out=ssq[:, ct, k:k + 1])

        def maxi(k, ct):
            g, mb = divmod(k, BPG)
            z = zts[(k, ct)]
            if mb == 0:
                nc.vector.tensor_copy(out=rmax[g][:, ct, :], in_=z[:])
            else:
                nc.vector.tensor_tensor(out=rmax[g][:, ct, :], in0=z[:], in1=rmax[g][:, ct, :], op=ALU.max)

        a1s = [keep.tile([P, 4, 256], BF16, name="a1_%d" % g) for g in range(2)]

        def group_a_step(g, step):
            a1 = a1s[g]
            if step == 0:
                nc.vector.tensor_tensor(out=a1[:], in0=arun[g][:, :, 0:256], in1=arun[g][:, :, 256:512], op=ALU.max)
            elif step == 1:
                nc.vector.tensor_tensor(out=agr[:, g, :].rearrange("p (n t) -> p n t", t=4),
                                        in0=a1[:, :, 0:128].rearrange("p t n -> p n t"),
                                        in1=a1[:, :, 128:256].rearrange("p t n -> p n t"), op=ALU.max)
            else:
                nc.vector.quantize_mx(out=ac[:, g, :].bitcast(FP8X4), scales=asc[:, g, :], in_=agr[:, g, :])

        def group_a(g):
            for step in range(3):
                group_a_step(g, step)

        def group_zs_copy(g):
            nc.scalar.copy(out=zs_sb[g][:], in_=zsum[g][:])

        def group_zs_transposes(g):
            zstp[g] = ps_d([P, 4, P], F32, "zst_ps")
            for ct in range(4):
                nc.tensor.transpose(zstp[g][:, ct, :], zs_sb[g][:, ct * P:(ct + 1) * P], ident_f[:])

        def group_zs_sums(g):
            for ct in range(4):
                nc.scalar.activation(out=zst_sb[:, ct, g, :], in_=zstp[g][:, ct, :], func=ACT.Copy, scale=1.0 / NPTS, accum_out=lsum[:, g, ct:ct + 1])

        def group_u_copies(g):
            for ct in range(4):
                nc.scalar.activation(out=u_sb[:, ct, g, :], in_=uts[g][:, ct, :], func=ACT.Copy, scale=sgn[:, ct:ct + 1], accum_out=lsum[:, 2 + g, ct:ct + 1])

        def group_u_squares(g):
            for ct in range(4):
                junk_b = work.tile([P, P], BF16, name="junk_b")
                nc.scalar.activation(out=junk_b[:], in_=uts[g][:, ct, :], func=ACT.Square, scale=8.0, accum_out=ssq[:, ct, NBLK + g:NBLK + g + 1])

        def cross_sums():
            for ct in range(4):
                junk_c = work.tile([P, 256], BF16, name="junk_c")
                nc.scalar.activation(out=junk_c[:], in_=prod[:, ct, :, :].rearrange("p g n -> p (g n)"), func=ACT.Copy, scale=2.0 * NPTS, accum_out=ssq[:, ct, NBLK + 2:NBLK + 3])

        def group_rm(g, step):
            if step == 0:
                nc.vector.tensor_tensor(out=rh[:], in0=rmax[g][:, :, 0:256], in1=rmax[g][:, :, 256:512], op=ALU.max)
            else:
                nc.vector.tensor_tensor(out=rm[:, :, g, :], in0=rh[:, :, 0:128], in1=rh[:, :, 128:256], op=ALU.max)

        uts = {}

        def u_passes(g):
            uts[g] = ps_a([P, 4, P], F32, "ut")
            for ct in range(4):
                nc.tensor.matmul_mx(out=uts[g][:, ct, :], lhsT=w1c[:, 1, ct * P:(ct + 1) * P].bitcast(FP8X4),
                                    lhsT_scale=w1s[:, 1, ct * P:(ct + 1) * P],
                                    rhs=ac[:, g, :].bitcast(FP8X4), rhs_scale=asc[:, g, :], start=True, stop=True)

        for t in range(4):
            l0(0, t)
        for t in range(4):
            affine(0, t)
        xt_copy(3, "vector")
        w1_quantise(0)
        regroup(0)
        amax(0)
        quantise(0)
        for t in range(4):
            l0(1, t)
        for t in range(4):
            affine(1, t)
        for t in range(4):
            l0(2, t)
        l0(3, 0)
        l0(3, 1)
        xt_transposes(4)
        xt_copy(4, "vector")
        regroup(1)
        amax(1)
        quantise(1)
        affine(2, 0)
        affine(2, 1)
        affine(2, 2)
        l0(3, 2)
        affine(2, 3)
        l0(3, 3)
        regroup(2)
        z_pass(0, 0)
        z_pass(0, 1)
        xt_transposes(5)
        xt_copy(5, "vector")
        affine(3, 0)
        affine(3, 1)
        affine(3, 2)
        l0(4, 0)
        affine(3, 3)
        l0(4, 1)
        zsum_passes(0)

        def have(k):
            return k < NBLK

        for i in range(NBLK - 4):
            if i >= 1:
                quantise(i + 1)
            regroup(i + 3)
            if i >= 1:
                amax(i + 1)
            affine(i + 4, 0)
            square(i, 0)
            z_pass(i, 2)
            l0(i + 4, 2)
            affine(i + 4, 1)
            square(i, 1)
            z_pass(i, 3)
            if have(i + 6):
                xt_transposes(i + 6)
            l0(i + 4, 3)
            zsum_passes(i + 1)
            maxi(i, 0)
            affine(i + 4, 2)
            square(i, 2)
            if have(i + 5):
                l0(i + 5, 0)
            z_pass(i + 1, 0)
            maxi(i, 1)
            affine(i + 4, 3)
            square(i, 3)
            if i == BPG - 2:
                group_zs_copy(0)
            if have(i + 5):
                l0(i + 5, 1)
            z_pass(i + 1, 1)
            maxi(i, 2)
            if have(i + 6):
                xt_copy(i + 6, "vector")
            maxi(i, 3)
            if BPG <= i < BPG + 2:
                group_rm(0, i - BPG)
            if GA0 <= i < GA0 + 3:
                group_a_step(0, i - GA0)

        i = NBLK - 4
        quantise(i + 1)
        regroup(i + 3)
        amax(i + 1)
        square(i, 0)
        z_pass(i, 2)
        square(i, 1)
        z_pass(i, 3)
        w1_transposes(1, 0)
        w1_transposes(1, 1)
        group_zs_transposes(0)
        zsum_passes(i + 1)
        maxi(i, 0)
        square(i, 2)
        z_pass(i + 1, 0)
        maxi(i, 1)
        square(i, 3)
        w1_copy(1, 0)
        w1_copy(1, 1)
        group_zs_sums(0)
        z_pass(i + 1, 1)
        maxi(i, 2)
        maxi(i, 3)

        i = NBLK - 3
        w1_quantise(1)
        quantise(i + 1)
        amax(i + 1)
        square(i, 0)
        z_pass(i, 2)
        square(i, 1)
        z_pass(i, 3)
        u_passes(0)
        zsum_passes(i + 1)
        maxi(i, 0)
        square(i, 2)
        z_pass(i + 1, 0)
        maxi(i, 1)
        square(i, 3)
        group_u_copies(0)
        nc.gpsimd.tensor_tensor(out=tmx[:, :, 0, :], in0=rm[:, :, 0, :], in1=u_sb[:, :, 0, :], op=ALU.add)
        group_u_squares(0)
        z_pass(i + 1, 1)
        maxi(i, 2)
        maxi(i, 3)

        i = NBLK - 2
        quantise(i + 1)
        amax(i + 1)
        group_a(1)
        square(i, 0)
        z_pass(i, 2)
        square(i, 1)
        z_pass(i, 3)
        zsum_passes(i + 1)
        square(i, 2)
        square(i, 3)
        group_zs_copy(1)
        group_zs_transposes(1)
        group_zs_sums(1)
        u_passes(1)
        group_u_copies(1)
        nc.gpsimd.tensor_tensor(out=prod[:], in0=u_sb[:], in1=zst_sb[:], op=ALU.mult)
        maxi(i, 0)
        z_pass(i + 1, 0)
        maxi(i, 1)
        z_pass(i + 1, 1)
        maxi(i, 2)
        z_pass(i + 1, 2)
        maxi(i, 3)
        z_pass(i + 1, 3)

        def small(name):
            return keep.tile([P, 4], F32, name=name)

        i = NBLK - 1
        for ct in range(4):
            square(i, ct)
            maxi(i, ct)
        group_u_squares(1)
        cross_sums()
        linp = small("linp")
        msq1 = small("msq1")
        negm = small("negm")
        q1 = small("q1")
        var1 = small("var1")
        rstd1 = small("rstd1")
        s1 = small("s1")
        b1 = small("b1")
        nc.vector.tensor_reduce(out=linp[:], in_=lsum[:].rearrange("p r c -> p c r"), axis=AX.X, op=ALU.add)
        group_rm(1, 0)
        nc.vector.scalar_tensor_tensor(out=msq1[:], in0=linp[:], scalar=(float(NPTS) / ROWS) * (float(NPTS) / ROWS), in1=linp[:], op0=ALU.mult, op1=ALU.mult)
        nc.vector.scalar_tensor_tensor(out=negm[:], in0=linp[:], scalar=-float(NPTS) / ROWS, in1=gabs[:], op0=ALU.mult, op1=ALU.mult)
        group_rm(1, 1)
        nc.vector.tensor_scalar(out=msq1[:], in0=msq1[:], scalar1=EPS, scalar2=None, op0=ALU.subtract)
        nc.vector.tensor_reduce(out=q1[:], in_=ssq[:], axis=AX.X, op=ALU.add)
        nc.vector.scalar_tensor_tensor(out=var1[:], in0=q1[:], scalar=1.0 / ROWS, in1=msq1[:], op0=ALU.mult, op1=ALU.subtract)
        nc.scalar.activation(out=rstd1[:], in_=var1[:], func=ACT.Abs_reciprocal_sqrt)
        nc.vector.tensor_tensor(out=tmx[:, :, 1, :], in0=rm[:, :, 1, :], in1=u_sb[:, :, 1, :], op=ALU.add)
        nc.vector.scalar_tensor_tensor(out=b1[:], in0=rstd1[:], scalar=RMAX, in1=negm[:], op0=ALU.min, op1=ALU.mult)
        nc.vector.scalar_tensor_tensor(out=s1[:], in0=rstd1[:], scalar=RMAX, in1=gabs[:], op0=ALU.min, op1=ALU.mult)
        nc.vector.tensor_tensor(out=b1[:], in0=b1[:], in1=gb1[:, 4:8], op=ALU.add)

        fin = keep.tile([P, 4, 2, P], F32, name="fin")
        for ct in range(4):
            if ct < 1:
                nc.scalar.activation(out=fin[:, ct, :, :], in_=tmx[:, ct, :, :], func=ACT.Identity, bias=b1[:, ct:ct + 1], scale=s1[:, ct:ct + 1])
            else:
                nc.vector.tensor_scalar(out=fin[:, ct, :, :], in0=tmx[:, ct, :, :], scalar1=s1[:, ct:ct + 1], scalar2=b1[:, ct:ct + 1],
                                        op0=ALU.mult, op1=ALU.add)
        for g in range(2):
            o_ps = ps_b([P, 512], F32, "o_ps")
            for ct in (1, 2, 3, 0):
                nc.tensor.transpose(o_ps[:, ct * P:(ct + 1) * P], fin[:, ct, g, :], ident_f[:])
            for half in (1, 0):
                cols = slice(256 * half, 256 * half + 256)
                o_sb = work.tile([P, 256], F32, name="o_sb%d" % half, bufs=2)
                if g == 0:
                    nc.scalar.activation(out=o_sb[:], in_=o_ps[:, cols], func=ACT.Relu)
                    nc.sync.dma_start(out=out[g * P:(g + 1) * P, cols], in_=o_sb[:])
                else:
                    nc.vector.tensor_scalar(out=o_sb[:], in0=o_ps[:, cols], scalar1=0.0, scalar2=None, op0=ALU.max)
                    nc.scalar.dma_start(out=out[g * P:(g + 1) * P, cols], in_=o_sb[:])
